import numpy as np
import ml_dtypes


def mxq(x, axis, fmt="e4m3"):
    dtype, down = {"e4m3": (ml_dtypes.float8_e4m3fn, 7), "e5m2": (ml_dtypes.float8_e5m2, 14)}[fmt]
    v = np.moveaxis(np.asarray(x, np.float32).astype(ml_dtypes.bfloat16).astype(np.float64), axis, -1)
    blocks = v.reshape(v.shape[:-1] + (-1, 32))
    amax = np.abs(blocks).max(-1, keepdims=True)
    byte = np.maximum(np.where(amax > 0, np.frexp(amax)[1] - 1 + 127, 0) - down, 1)
    scale = np.exp2(byte - 127.0)
    codes = (blocks / scale).astype(np.float32).astype(dtype).astype(np.float64)
    return np.moveaxis((codes * scale).reshape(v.shape), -1, axis)


WIDE = False


def mx_kscale(k):
    if not WIDE:
        return np.ones(k)
    levels = np.array([10, -10, 5, -5, 0])
    a = np.random.permutation(np.resize(levels, k // 512 * 4)).reshape(k // 512, 4)
    idx = np.arange(k)
    return np.exp2(a[idx // 512, idx % 128 // 32])


BF16 = ml_dtypes.bfloat16


def bf(x):
    return np.asarray(x, np.float32).astype(BF16)


def f64(x):
    return np.asarray(x).astype(np.float64)


E2M1 = np.array([0.0, 0.5, 1.0, 1.5, 2.0, 3.0, 4.0, 6.0, -0.0, -0.5, -1.0, -1.5, -2.0, -3.0, -4.0, -6.0])


def pack_weight(w, fmt):
    k, n = w.shape
    w = f64(bf(w)).reshape(k // 32, 32, n)
    amax = np.abs(w).max(1)
    if fmt == "e4m3":
        byte = np.frexp(amax)[1] - 1 + 127 - 7
    else:
        mant, ex = np.frexp(amax / 6.0)
        byte = np.where(mant > 0.5, ex, ex - 1) + 127
    byte = np.clip(np.where(amax > 0, byte, 1), 1, 254)
    scaled = (w * np.exp2(127.0 - byte)[:, None, :]).reshape(k, n).astype(np.float32)
    by_word = np.ascontiguousarray(scaled.reshape(k // 512, 128, 4, n).transpose(0, 1, 3, 2))
    if fmt == "e4m3":
        words = by_word.astype(ml_dtypes.float8_e4m3fn).view(np.uint8)
    else:
        c = by_word.astype(ml_dtypes.float4_e2m1fn).view(np.uint8) & 0xF
        words = c[..., 0::2] | (c[..., 1::2] << 4)
    return np.ascontiguousarray(words), np.ascontiguousarray(byte.astype(np.uint8).reshape(k // 512, 16, n))


def unpack_weight(words, scales, fmt):
    g, p, n, _ = words.shape
    if fmt == "e4m3":
        vals = np.ascontiguousarray(words).view(ml_dtypes.float8_e4m3fn).astype(np.float64)
    else:
        nib = np.empty((g, p, n, 4), np.uint8)
        nib[..., 0::2] = words & 0xF
        nib[..., 1::2] = words >> 4
        vals = E2M1[nib]
    vals = vals * np.repeat(np.exp2(scales.astype(np.float64) - 127.0), 8, axis=1)[..., None]
    return vals.transpose(0, 1, 3, 2).reshape(g * 512, n)

def pack4(w):
    words, scales = pack_weight(w, "e2m1")
    return words.reshape(words.shape[0], 128, -1), scales


def unpack4(words, scales):
    return unpack_weight(words.reshape(words.shape[0], 128, -1, 2), scales, "e2m1")


B, IN, H = 512, 1024, 1024


def sigmoid(v):
    return 1.0 / (1.0 + np.exp(-v))


def setup_inputs():
    s, t = mx_kscale(IN), mx_kscale(H)
    a = np.sqrt(2.0 / (IN + H))
    x = bf(np.random.standard_normal((B, IN)) * s)
    h_prev = bf(np.random.standard_normal((B, H)) * t)
    m_prev = bf(np.random.standard_normal((B, H)) * 0.5)
    Wi_x_words, Wi_x_scales = pack4((np.random.standard_normal((H, IN)) * a / s).T)
    b_i = bf(np.random.standard_normal(H) * 0.3)
    Wi_h_words, Wi_h_scales = pack4((np.random.standard_normal((H, H)) * a / t).T)
    Wf_x_words, Wf_x_scales = pack4((np.random.standard_normal((H, IN)) * a / s).T)
    b_f = bf(2.0 + np.random.standard_normal(H) * 0.3)
    Wf_h_words, Wf_h_scales = pack4((np.random.standard_normal((H, H)) * a / t).T)
    return {
        "x": x,
        "h_prev": h_prev,
        "m_prev": m_prev,
        "Wi_x_words": Wi_x_words,
        "Wi_x_scales": Wi_x_scales,
        "b_i": b_i,
        "Wi_h_words": Wi_h_words,
        "Wi_h_scales": Wi_h_scales,
        "Wf_x_words": Wf_x_words,
        "Wf_x_scales": Wf_x_scales,
        "b_f": b_f,
        "Wf_h_words": Wf_h_words,
        "Wf_h_scales": Wf_h_scales,
    }


def reference(x, h_prev, m_prev, Wi_x_words, Wi_x_scales, b_i, Wi_h_words, Wi_h_scales, Wf_x_words, Wf_x_scales, b_f, Wf_h_words, Wf_h_scales):
    xq = mxq(f64(x), 1, "e4m3")
    hq = mxq(f64(h_prev), 1, "e4m3")
    i_tilde = (xq @ unpack4(Wi_x_words, Wi_x_scales)) + f64(b_i) + (hq @ unpack4(Wi_h_words, Wi_h_scales))
    f_aff = (xq @ unpack4(Wf_x_words, Wf_x_scales)) + f64(b_f) + (hq @ unpack4(Wf_h_words, Wf_h_scales))
    log_f = np.log(np.maximum(sigmoid(f_aff), 1e-8))
    m_t = np.maximum(log_f + f64(m_prev), i_tilde)
    i_prime = np.exp(i_tilde - m_t)
    f_prime = np.exp(log_f + f64(m_prev) - m_t)
    return m_t, i_prime, f_prime

@@ -1,0 +1,227 @@
+import math
+from contextlib import ExitStack
+
+import concourse.mybir as mybir
+from concourse.masks import make_identity
+
+F32 = mybir.dt.float32
+BF16 = mybir.dt.bfloat16
+I32 = mybir.dt.int32
+U32 = mybir.dt.uint32
+U8 = mybir.dt.uint8
+FP8X4 = mybir.dt.float8_e4m3fn_x4
+FP4X4 = mybir.dt.float4_e2m1fn_x4
+ACT = mybir.ActivationFunctionType
+ALU = mybir.AluOpType
+
+P = 128
+BATCH = 512
+FEATURES = 1024
+HIDDEN = 1024
+K_PASS = 4 * P
+BATCH_TILES = BATCH // P
+GROUPS = FEATURES // K_PASS
+PASSES = 2 * GROUPS
+N_TILE = 512
+N_HALVES = HIDDEN // N_TILE
+WORDS_PER_GROUP = K_PASS // 2
+F_GATE, I_GATE = 0, 1
+CHUNKS = ((0, 1), (2, 3))
+
+SIGMOID_FLOOR = 1e-8
+LOG_FLOOR = math.log(SIGMOID_FLOOR)
+LN_GUARD = 1e-18
+
+FLOPS = 2 * BATCH * (2 * FEATURES) * (2 * HIDDEN)
+
+
+def tile_slstmlayer_pa_kernel(
+    tc,
+    x,
+    h_prev,
+    m_prev,
+    Wi_x_words,
+    Wi_x_scales,
+    b_i,
+    Wi_h_words,
+    Wi_h_scales,
+    Wf_x_words,
+    Wf_x_scales,
+    b_f,
+    Wf_h_words,
+    Wf_h_scales,
+    out_0,
+    out_1,
+    out_2,
+):
+    nc = tc.nc
+    with ExitStack() as ctx:
+        keep = ctx.enter_context(tc.tile_pool(name="keep", bufs=1))
+        stage = ctx.enter_context(tc.tile_pool(name="stage", bufs=4))
+        work = ctx.enter_context(tc.tile_pool(name="work", bufs=4))
+        psum_t = ctx.enter_context(tc.psum_pool(name="psum_t", bufs=2))
+        psum_acc = ctx.enter_context(tc.psum_pool(name="psum_acc", bufs=6))
+        ctx.enter_context(tc.manual_schedule())
+
+        x_sb = keep.tile([P, BATCH_TILES, FEATURES], BF16)
+        h_sb = keep.tile([P, BATCH_TILES, FEATURES], BF16)
+        m_sb = keep.tile([P, BATCH_TILES, HIDDEN], BF16)
+        w_words = keep.tile([P, 2 * PASSES, 2 * HIDDEN], U8, align_bytes=64)
+        w_scales = keep.tile([P, 2 * PASSES, HIDDEN], U8, align_bytes=64)
+        a_codes = keep.tile([P, BATCH_TILES, PASSES, P], U32, align_bytes=64)
+        a_scales = keep.tile([P, BATCH_TILES, PASSES, P], U8, align_bytes=64)
+        bias_rows = keep.tile([P, 2, HIDDEN], BF16)
+        bias_all = keep.tile([P, 2, HIDDEN], F32)
+        ones = keep.tile([P, P], BF16)
+        ident = keep.tile([P, P], F32)
+        ln_guard = keep.tile([P, 1], F32)
+        sig_f = keep.tile([P, BATCH_TILES, HIDDEN], F32)
+        f_path = keep.tile([P, BATCH_TILES, HIDDEN], F32)
+        below = keep.tile([P, BATCH_TILES, HIDDEN], F32)
+        above = keep.tile([P, BATCH_TILES, HIDDEN], F32)
+        m_t = keep.tile([P, BATCH_TILES, HIDDEN], F32)
+        i_prime = keep.tile([P, BATCH_TILES, HIDDEN], F32)
+        f_prime = keep.tile([P, BATCH_TILES, HIDDEN], F32)
+
+        nc.vector.memset(w_scales[:].rearrange("p s n -> p (s n)").bitcast(I32), 0)
+        nc.vector.memset(bias_rows[:].rearrange("p g n -> p (g n)").bitcast(I32), 0)
+        nc.vector.memset(ones[:], 1.0)
+        nc.vector.memset(ln_guard[:], LN_GUARD)
+        make_identity(nc, ident[:])
+
+        nc.scalar.dma_start(out=bias_rows[0:1, F_GATE, :], in_=b_f.rearrange("(o n) -> o n", o=1))
+        nc.scalar.dma_start(out=bias_rows[0:1, I_GATE, :], in_=b_i.rearrange("(o n) -> o n", o=1))
+        for bt in range(BATCH_TILES):
+            nc.sync.dma_start(out=x_sb[:, bt, :], in_=x[bt * P : (bt + 1) * P, :])
+            nc.sync.dma_start(out=h_sb[:, bt, :], in_=h_prev[bt * P : (bt + 1) * P, :])
+        gate_weights = (
+            ((Wf_x_words, Wf_x_scales), (Wf_h_words, Wf_h_scales)),
+            ((Wi_x_words, Wi_x_scales), (Wi_h_words, Wi_h_scales)),
+        )
+        for gate in (F_GATE, I_GATE):
+            for operand, (words, scales) in enumerate(gate_weights[gate]):
+                slot = gate * PASSES + operand * GROUPS
+                for q in range(8):
+                    part = 32 * (q // 4) + q % 4
+                    nc.sync.dma_start(
+                        out=w_scales[part : P : 64, slot : slot + GROUPS, :].bitcast(I32),
+                        in_=scales[:, q : 16 : 8, :].rearrange("g q n -> q g n").bitcast(I32),
+                    )
+            for operand, (words, scales) in enumerate(gate_weights[gate]):
+                for g in range(GROUPS):
+                    slot = gate * PASSES + operand * GROUPS + g
+                    nc.sync.dma_start(out=w_words[:, slot, :].bitcast(I32), in_=words[g].bitcast(I32))
+        for bt in range(BATCH_TILES):
+            nc.sync.dma_start(out=m_sb[:, bt, :], in_=m_prev[bt * P : (bt + 1) * P, :])
+
+        def turn(act_sb, bt, copy_out):
+            row_words = act_sb[:, bt, :].bitcast(F32)
+            turned = psum_t.tile([P, GROUPS, 2, P], F32)
+            for g in range(GROUPS):
+                for u in range(2):
+                    nc.tensor.transpose(
+                        out=turned[:, g, u, :],
+                        in_=row_words[:, WORDS_PER_GROUP * g + u : WORDS_PER_GROUP * (g + 1) : 2],
+                        identity=ident[:],
+                    )
+            grouped = stage.tile([P, GROUPS * P * 4], BF16, align_bytes=64)
+            copy_out(
+                out=grouped[:].bitcast(F32).rearrange("p (g b u) -> p g b u", g=GROUPS, u=2),
+                in_=turned[:].rearrange("p g u b -> p g b u"),
+            )
+            return grouped
+
+        def quantise(grouped, bt, operand):
+            passes = slice(operand * GROUPS, (operand + 1) * GROUPS)
+            nc.vector.quantize_mx(
+                out=a_codes[:, bt, passes, :].rearrange("p g b -> p (g b)").bitcast(FP8X4),
+                scales=a_scales[:, bt, passes, :].rearrange("p g b -> p (g b)"),
+                in_=grouped[:],
+            )
+
+        waiting = []
+        for bt in range(BATCH_TILES):
+            turned_now = [(turn(x_sb, bt, nc.scalar.copy), bt, 0), (turn(h_sb, bt, nc.vector.tensor_copy), bt, 1)]
+            for item in waiting:
+                quantise(*item)
+            waiting = turned_now
+        for item in waiting:
+            quantise(*item)
+
+        for gate in (F_GATE, I_GATE):
+            for nh in range(N_HALVES):
+                cols = slice(nh * N_TILE, (nh + 1) * N_TILE)
+                spread = psum_acc.tile([P, N_TILE], F32, tag="acc")
+                nc.tensor.matmul(out=spread[:], lhsT=ones[:], rhs=bias_rows[:, gate, cols], start=True, stop=True)
+                nc.scalar.copy(out=bias_all[:, gate, cols], in_=spread[:])
+
+        halves = [slice(nh * N_TILE, (nh + 1) * N_TILE) for nh in range(N_HALVES)]
+
+        def gate_products(gate, bt):
+            banks = [psum_acc.tile([P, N_TILE], F32, name="acc%d" % nh, tag="acc") for nh in range(N_HALVES)]
+            for ps in range(PASSES):
+                for nh in range(N_HALVES):
+                    nc.tensor.matmul_mx(
+                        out=banks[nh][:],
+                        lhsT=a_codes[:, bt, ps, :].bitcast(FP8X4),
+                        lhsT_scale=a_scales[:, bt, ps, :],
+                        rhs=w_words[:, gate * PASSES + ps, 2 * nh * N_TILE : 2 * (nh + 1) * N_TILE].bitcast(FP4X4),
+                        rhs_scale=w_scales[:, gate * PASSES + ps, nh * N_TILE : (nh + 1) * N_TILE],
+                        start=(ps == 0),
+                        stop=(ps == PASSES - 1),
+                    )
+            return banks
+
+        def forget_sigmoids(chunk):
+            for bt in chunk:
+                banks = gate_products(F_GATE, bt)
+                for nh, cols in enumerate(halves):
+                    f_aff = work.tile([P, N_TILE], F32)
+                    nc.vector.tensor_tensor(out=f_aff[:], in0=banks[nh][:], in1=bias_all[:, F_GATE, cols], op=ALU.add)
+                    nc.scalar.activation(out=sig_f[:, bt, cols], in_=f_aff[:], func=ACT.Sigmoid)
+
+        def forget_paths(chunk):
+            for bt in chunk:
+                for cols in halves:
+                    log_s = work.tile([P, N_TILE], F32)
+                    nc.scalar.activation(out=log_s[:], in_=sig_f[:, bt, cols], func=ACT.Ln, bias=ln_guard[:, 0:1])
+                    nc.vector.scalar_tensor_tensor(
+                        out=f_path[:, bt, cols],
+                        in0=log_s[:],
+                        scalar=LOG_FLOOR,
+                        in1=m_sb[:, bt, cols],
+                        op0=ALU.max,
+                        op1=ALU.add,
+                    )
+
+        def stabilise(chunk):
+            for bt in chunk:
+                banks = gate_products(I_GATE, bt)
+                i_tilde = [work.tile([P, N_TILE], F32, name="i_tilde") for nh in range(N_HALVES)]
+                diff = [work.tile([P, N_TILE], F32, name="diff") for nh in range(N_HALVES)]
+                for nh, cols in enumerate(halves):
+                    nc.vector.tensor_tensor(out=i_tilde[nh][:], in0=banks[nh][:], in1=bias_all[:, I_GATE, cols], op=ALU.add)
+                for nh, cols in enumerate(halves):
+                    nc.vector.tensor_tensor(out=diff[nh][:], in0=i_tilde[nh][:], in1=f_path[:, bt, cols], op=ALU.subtract)
+                for nh, cols in enumerate(halves):
+                    nc.vector.tensor_scalar_min(out=below[:, bt, cols], in0=diff[nh][:], scalar1=0.0)
+                for nh, cols in enumerate(halves):
+                    nc.vector.tensor_scalar_max(out=above[:, bt, cols], in0=diff[nh][:], scalar1=0.0)
+                for nh, cols in enumerate(halves):
+                    nc.vector.tensor_tensor(out=m_t[:, bt, cols], in0=i_tilde[nh][:], in1=f_path[:, bt, cols], op=ALU.max)
+                    nc.sync.dma_start(out=out_0[bt * P : (bt + 1) * P, cols], in_=m_t[:, bt, cols])
+
+        forget_sigmoids(CHUNKS[0])
+        for c, chunk in enumerate(CHUNKS):
+            forget_paths(chunk)
+            if c + 1 < len(CHUNKS):
+                forget_sigmoids(CHUNKS[c + 1])
+            stabilise(chunk)
+        for bt in range(BATCH_TILES):
+            rows = slice(bt * P, (bt + 1) * P)
+            for cols in halves:
+                nc.scalar.activation(out=i_prime[:, bt, cols], in_=below[:, bt, cols], func=ACT.Exp)
+                nc.scalar.dma_start(out=out_1[rows, cols], in_=i_prime[:, bt, cols])
+            for cols in halves:
+                nc.scalar.activation(out=f_prime[:, bt, cols], in_=above[:, bt, cols], func=ACT.Exp, scale=-1.0)
+                nc.scalar.dma_start(out=out_2[rows, cols], in_=f_prime[:, bt, cols])

@@ -58,7 +58,7 @@ def tile_slstmlayer_pa_kernel(
     with ExitStack() as ctx:
         keep = ctx.enter_context(tc.tile_pool(name="keep", bufs=1))
         stage = ctx.enter_context(tc.tile_pool(name="stage", bufs=4))
-        work = ctx.enter_context(tc.tile_pool(name="work", bufs=4))
+        work = ctx.enter_context(tc.tile_pool(name="work", bufs=2))
         psum_t = ctx.enter_context(tc.psum_pool(name="psum_t", bufs=2))
         psum_acc = ctx.enter_context(tc.psum_pool(name="psum_acc", bufs=6))
         ctx.enter_context(tc.manual_schedule())
@@ -89,30 +89,35 @@ def tile_slstmlayer_pa_kernel(
         nc.vector.memset(ln_guard[:], LN_GUARD)
         make_identity(nc, ident[:])
 
+        def load_rows(tile_sb, source, chunk):
+            first, last = chunk[0], chunk[-1] + 1
+            nc.sync.dma_start(
+                out=tile_sb[:, first:last, :],
+                in_=source[first * P : last * P, :].rearrange("(t p) k -> p t k", p=P),
+            )
+
+        def load_weight(gate, operand, words, scales):
+            slot = gate * PASSES + operand * GROUPS
+            for r in range(4):
+                nc.sync.dma_start(
+                    out=w_scales[r : P : 32, slot : slot + GROUPS, :].bitcast(I32),
+                    in_=scales[:, r : 16 : 4, :].rearrange("g q n -> q g n").bitcast(I32),
+                )
+            for g in range(GROUPS):
+                nc.sync.dma_start(out=w_words[:, slot + g, :].bitcast(I32), in_=words[g].bitcast(I32))
+
         nc.scalar.dma_start(out=bias_rows[0:1, F_GATE, :], in_=b_f.rearrange("(o n) -> o n", o=1))
         nc.scalar.dma_start(out=bias_rows[0:1, I_GATE, :], in_=b_i.rearrange("(o n) -> o n", o=1))
-        for bt in range(BATCH_TILES):
-            nc.sync.dma_start(out=x_sb[:, bt, :], in_=x[bt * P : (bt + 1) * P, :])
-            nc.sync.dma_start(out=h_sb[:, bt, :], in_=h_prev[bt * P : (bt + 1) * P, :])
-        gate_weights = (
-            ((Wf_x_words, Wf_x_scales), (Wf_h_words, Wf_h_scales)),
-            ((Wi_x_words, Wi_x_scales), (Wi_h_words, Wi_h_scales)),
-        )
-        for gate in (F_GATE, I_GATE):
-            for operand, (words, scales) in enumerate(gate_weights[gate]):
-                slot = gate * PASSES + operand * GROUPS
-                for q in range(8):
-                    part = 32 * (q // 4) + q % 4
-                    nc.sync.dma_start(
-                        out=w_scales[part : P : 64, slot : slot + GROUPS, :].bitcast(I32),
-                        in_=scales[:, q : 16 : 8, :].rearrange("g q n -> q g n").bitcast(I32),
-                    )
-            for operand, (words, scales) in enumerate(gate_weights[gate]):
-                for g in range(GROUPS):
-                    slot = gate * PASSES + operand * GROUPS + g
-                    nc.sync.dma_start(out=w_words[:, slot, :].bitcast(I32), in_=words[g].bitcast(I32))
-        for bt in range(BATCH_TILES):
-            nc.sync.dma_start(out=m_sb[:, bt, :], in_=m_prev[bt * P : (bt + 1) * P, :])
+        load_rows(x_sb, x, CHUNKS[0])
+        load_rows(h_sb, h_prev, CHUNKS[0])
+        load_weight(F_GATE, 0, Wf_x_words, Wf_x_scales)
+        load_weight(F_GATE, 1, Wf_h_words, Wf_h_scales)
+        load_rows(x_sb, x, CHUNKS[1])
+        load_rows(h_sb, h_prev, CHUNKS[1])
+        load_weight(I_GATE, 0, Wi_x_words, Wi_x_scales)
+        load_weight(I_GATE, 1, Wi_h_words, Wi_h_scales)
+        load_rows(m_sb, m_prev, CHUNKS[0])
+        load_rows(m_sb, m_prev, CHUNKS[1])
 
         def turn(act_sb, bt, copy_out):
             row_words = act_sb[:, bt, :].bitcast(F32)
@@ -139,14 +144,14 @@ def tile_slstmlayer_pa_kernel(
                 in_=grouped[:],
             )
 
-        waiting = []
-        for bt in range(BATCH_TILES):
-            turned_now = [(turn(x_sb, bt, nc.scalar.copy), bt, 0), (turn(h_sb, bt, nc.vector.tensor_copy), bt, 1)]
-            for item in waiting:
-                quantise(*item)
-            waiting = turned_now
-        for item in waiting:
-            quantise(*item)
+        def quantise_chunk(chunk, x_copy_out):
+            turned_x = [turn(x_sb, bt, x_copy_out) for bt in chunk]
+            turned_h = [turn(h_sb, bt, nc.vector.tensor_copy) for bt in chunk]
+            for j, bt in enumerate(chunk):
+                quantise(turned_x[j], bt, 0)
+                quantise(turned_h[j], bt, 1)
+
+        quantise_chunk(CHUNKS[0], nc.scalar.copy)
 
         for gate in (F_GATE, I_GATE):
             for nh in range(N_HALVES):
@@ -175,53 +180,57 @@ def tile_slstmlayer_pa_kernel(
         def forget_sigmoids(chunk):
             for bt in chunk:
                 banks = gate_products(F_GATE, bt)
+                f_aff = work.tile([P, HIDDEN], F32)
                 for nh, cols in enumerate(halves):
-                    f_aff = work.tile([P, N_TILE], F32)
-                    nc.vector.tensor_tensor(out=f_aff[:], in0=banks[nh][:], in1=bias_all[:, F_GATE, cols], op=ALU.add)
-                    nc.scalar.activation(out=sig_f[:, bt, cols], in_=f_aff[:], func=ACT.Sigmoid)
+                    nc.vector.tensor_tensor(out=f_aff[:, cols], in0=banks[nh][:], in1=bias_all[:, F_GATE, cols], op=ALU.add)
+                nc.scalar.activation(out=sig_f[:, bt, :], in_=f_aff[:], func=ACT.Sigmoid)
 
         def forget_paths(chunk):
             for bt in chunk:
+                log_s = work.tile([P, HIDDEN], F32)
+                nc.scalar.activation(out=log_s[:], in_=sig_f[:, bt, :], func=ACT.Ln, bias=ln_guard[:, 0:1])
                 for cols in halves:
-                    log_s = work.tile([P, N_TILE], F32)
-                    nc.scalar.activation(out=log_s[:], in_=sig_f[:, bt, cols], func=ACT.Ln, bias=ln_guard[:, 0:1])
                     nc.vector.scalar_tensor_tensor(
                         out=f_path[:, bt, cols],
-                        in0=log_s[:],
+                        in0=log_s[:, cols],
                         scalar=LOG_FLOOR,
                         in1=m_sb[:, bt, cols],
                         op0=ALU.max,
                         op1=ALU.add,
                     )
 
-        def stabilise(chunk):
-            for bt in chunk:
-                banks = gate_products(I_GATE, bt)
-                i_tilde = [work.tile([P, N_TILE], F32, name="i_tilde") for nh in range(N_HALVES)]
-                diff = [work.tile([P, N_TILE], F32, name="diff") for nh in range(N_HALVES)]
-                for nh, cols in enumerate(halves):
-                    nc.vector.tensor_tensor(out=i_tilde[nh][:], in0=banks[nh][:], in1=bias_all[:, I_GATE, cols], op=ALU.add)
-                for nh, cols in enumerate(halves):
-                    nc.vector.tensor_tensor(out=diff[nh][:], in0=i_tilde[nh][:], in1=f_path[:, bt, cols], op=ALU.subtract)
-                for nh, cols in enumerate(halves):
-                    nc.vector.tensor_scalar_min(out=below[:, bt, cols], in0=diff[nh][:], scalar1=0.0)
-                for nh, cols in enumerate(halves):
-                    nc.vector.tensor_scalar_max(out=above[:, bt, cols], in0=diff[nh][:], scalar1=0.0)
-                for nh, cols in enumerate(halves):
-                    nc.vector.tensor_tensor(out=m_t[:, bt, cols], in0=i_tilde[nh][:], in1=f_path[:, bt, cols], op=ALU.max)
-                    nc.sync.dma_start(out=out_0[bt * P : (bt + 1) * P, cols], in_=m_t[:, bt, cols])
+        def stabilise(bt):
+            banks = gate_products(I_GATE, bt)
+            i_tilde = work.tile([P, HIDDEN], F32)
+            diff = work.tile([P, HIDDEN], F32)
+            for nh, cols in enumerate(halves):
+                nc.vector.tensor_tensor(out=i_tilde[:, cols], in0=banks[nh][:], in1=bias_all[:, I_GATE, cols], op=ALU.add)
+            for cols in halves:
+                nc.vector.tensor_tensor(out=diff[:, cols], in0=i_tilde[:, cols], in1=f_path[:, bt, cols], op=ALU.subtract)
+            for cols in halves:
+                nc.vector.tensor_scalar_min(out=below[:, bt, cols], in0=diff[:, cols], scalar1=0.0)
+            for cols in halves:
+                nc.vector.tensor_scalar_max(out=above[:, bt, cols], in0=diff[:, cols], scalar1=0.0)
+            for cols in halves:
+                nc.vector.tensor_tensor(out=m_t[:, bt, cols], in0=i_tilde[:, cols], in1=f_path[:, bt, cols], op=ALU.max)
+            nc.sync.dma_start(out=out_0[bt * P : (bt + 1) * P, :], in_=m_t[:, bt, :])
+
+        def exponentials(bt):
+            rows = slice(bt * P, (bt + 1) * P)
+            nc.scalar.activation(out=i_prime[:, bt, :], in_=below[:, bt, :], func=ACT.Exp)
+            nc.sync.dma_start(out=out_1[rows, :], in_=i_prime[:, bt, :])
+            nc.scalar.activation(out=f_prime[:, bt, :], in_=above[:, bt, :], func=ACT.Exp, scale=-1.0)
+            nc.sync.dma_start(out=out_2[rows, :], in_=f_prime[:, bt, :])
 
         forget_sigmoids(CHUNKS[0])
-        for c, chunk in enumerate(CHUNKS):
-            forget_paths(chunk)
-            if c + 1 < len(CHUNKS):
-                forget_sigmoids(CHUNKS[c + 1])
-            stabilise(chunk)
-        for bt in range(BATCH_TILES):
-            rows = slice(bt * P, (bt + 1) * P)
-            for cols in halves:
-                nc.scalar.activation(out=i_prime[:, bt, cols], in_=below[:, bt, cols], func=ACT.Exp)
-                nc.scalar.dma_start(out=out_1[rows, cols], in_=i_prime[:, bt, cols])
-            for cols in halves:
-                nc.scalar.activation(out=f_prime[:, bt, cols], in_=above[:, bt, cols], func=ACT.Exp, scale=-1.0)
-                nc.scalar.dma_start(out=out_2[rows, cols], in_=f_prime[:, bt, cols])
+        quantise_chunk(CHUNKS[1], nc.vector.tensor_copy)
+        forget_paths(CHUNKS[0])
+        forget_sigmoids(CHUNKS[1])
+        for bt in CHUNKS[0]:
+            stabilise(bt)
+        forget_paths(CHUNKS[1])
+        for bt in CHUNKS[0]:
+            exponentials(bt)
+        for bt in CHUNKS[1]:
+            stabilise(bt)
+            exponentials(bt)

@@ -63,53 +63,61 @@ def tile_slstmlayer_pa_kernel(
         psum_acc = ctx.enter_context(tc.psum_pool(name="psum_acc", bufs=6))
         ctx.enter_context(tc.manual_schedule())
 
-        x_sb = keep.tile([P, BATCH_TILES, FEATURES], BF16)
-        h_sb = keep.tile([P, BATCH_TILES, FEATURES], BF16)
-        m_sb = keep.tile([P, BATCH_TILES, HIDDEN], BF16)
-        w_words = keep.tile([P, 2 * PASSES, 2 * HIDDEN], U8, align_bytes=64)
-        w_scales = keep.tile([P, 2 * PASSES, HIDDEN], U8, align_bytes=64)
-        a_codes = keep.tile([P, BATCH_TILES, PASSES, P], U32, align_bytes=64)
-        a_scales = keep.tile([P, BATCH_TILES, PASSES, P], U8, align_bytes=64)
+        def tiles_by_batch(name, width, dtype):
+            return [keep.tile([P, width], dtype, name="%s%d" % (name, bt), align_bytes=64) for bt in range(BATCH_TILES)]
+
+        x_sb = tiles_by_batch("x_sb", FEATURES, BF16)
+        h_sb = tiles_by_batch("h_sb", FEATURES, BF16)
+        m_sb = tiles_by_batch("m_sb", HIDDEN, BF16)
+        w_words = [
+            [keep.tile([P, GROUPS, 2 * HIDDEN], U8, name="w_words%d%d" % (gate, o), align_bytes=64) for o in range(2)]
+            for gate in range(2)
+        ]
+        w_scales = [
+            [keep.tile([P, GROUPS, HIDDEN], U8, name="w_scales%d%d" % (gate, o), align_bytes=64) for o in range(2)]
+            for gate in range(2)
+        ]
+        a_codes = tiles_by_batch("a_codes", PASSES * P, U32)
+        a_scales = tiles_by_batch("a_scales", PASSES * P, U8)
         bias_rows = keep.tile([P, 2, HIDDEN], BF16)
         bias_all = keep.tile([P, 2, HIDDEN], F32)
         ones = keep.tile([P, P], BF16)
         ident = keep.tile([P, P], F32)
         ln_guard = keep.tile([P, 1], F32)
-        sig_f = keep.tile([P, BATCH_TILES, HIDDEN], F32)
-        f_path = keep.tile([P, BATCH_TILES, HIDDEN], F32)
-        below = keep.tile([P, BATCH_TILES, HIDDEN], F32)
-        above = keep.tile([P, BATCH_TILES, HIDDEN], F32)
-        m_t = keep.tile([P, BATCH_TILES, HIDDEN], F32)
-        i_prime = keep.tile([P, BATCH_TILES, HIDDEN], F32)
-        f_prime = keep.tile([P, BATCH_TILES, HIDDEN], F32)
+        sig_f = tiles_by_batch("sig_f", HIDDEN, F32)
+        f_path = tiles_by_batch("f_path", HIDDEN, F32)
+        below = tiles_by_batch("below", HIDDEN, F32)
+        above = tiles_by_batch("above", HIDDEN, F32)
+        m_t = tiles_by_batch("m_t", HIDDEN, F32)
+        i_prime = tiles_by_batch("i_prime", HIDDEN, F32)
+        f_prime = tiles_by_batch("f_prime", HIDDEN, F32)
 
-        nc.vector.memset(w_scales[:].rearrange("p s n -> p (s n)").bitcast(I32), 0)
         nc.vector.memset(bias_rows[:].rearrange("p g n -> p (g n)").bitcast(I32), 0)
+        for gate in (F_GATE, I_GATE):
+            for planes in w_scales[gate]:
+                nc.vector.memset(planes[:].rearrange("p s n -> p (s n)").bitcast(I32), 0)
         nc.vector.memset(ones[:], 1.0)
         nc.vector.memset(ln_guard[:], LN_GUARD)
         make_identity(nc, ident[:])
 
-        def load_rows(tile_sb, source, chunk):
-            first, last = chunk[0], chunk[-1] + 1
-            nc.sync.dma_start(
-                out=tile_sb[:, first:last, :],
-                in_=source[first * P : last * P, :].rearrange("(t p) k -> p t k", p=P),
-            )
+        def load_rows(tiles_sb, source, chunk):
+            for bt in chunk:
+                nc.sync.dma_start(out=tiles_sb[bt][:], in_=source[bt * P : (bt + 1) * P, :])
 
         def load_weight(gate, operand, words, scales):
-            slot = gate * PASSES + operand * GROUPS
             for r in range(4):
                 nc.sync.dma_start(
-                    out=w_scales[r : P : 32, slot : slot + GROUPS, :].bitcast(I32),
+                    out=w_scales[gate][operand][r : P : 32, :, :].bitcast(I32),
                     in_=scales[:, r : 16 : 4, :].rearrange("g q n -> q g n").bitcast(I32),
                 )
-            for g in range(GROUPS):
-                nc.sync.dma_start(out=w_words[:, slot + g, :].bitcast(I32), in_=words[g].bitcast(I32))
+            nc.sync.dma_start(
+                out=w_words[gate][operand][:].bitcast(I32), in_=words.rearrange("g p c -> p g c").bitcast(I32)
+            )
 
-        nc.scalar.dma_start(out=bias_rows[0:1, F_GATE, :], in_=b_f.rearrange("(o n) -> o n", o=1))
-        nc.scalar.dma_start(out=bias_rows[0:1, I_GATE, :], in_=b_i.rearrange("(o n) -> o n", o=1))
         load_rows(x_sb, x, CHUNKS[0])
         load_rows(h_sb, h_prev, CHUNKS[0])
+        nc.sync.dma_start(out=bias_rows[0:1, F_GATE, :], in_=b_f.rearrange("(o n) -> o n", o=1))
+        nc.sync.dma_start(out=bias_rows[0:1, I_GATE, :], in_=b_i.rearrange("(o n) -> o n", o=1))
         load_weight(F_GATE, 0, Wf_x_words, Wf_x_scales)
         load_weight(F_GATE, 1, Wf_h_words, Wf_h_scales)
         load_rows(x_sb, x, CHUNKS[1])
@@ -120,7 +128,7 @@ def tile_slstmlayer_pa_kernel(
         load_rows(m_sb, m_prev, CHUNKS[1])
 
         def turn(act_sb, bt, copy_out):
-            row_words = act_sb[:, bt, :].bitcast(F32)
+            row_words = act_sb[bt][:].bitcast(F32)
             turned = psum_t.tile([P, GROUPS, 2, P], F32)
             for g in range(GROUPS):
                 for u in range(2):
@@ -137,12 +145,8 @@ def tile_slstmlayer_pa_kernel(
             return grouped
 
         def quantise(grouped, bt, operand):
-            passes = slice(operand * GROUPS, (operand + 1) * GROUPS)
-            nc.vector.quantize_mx(
-                out=a_codes[:, bt, passes, :].rearrange("p g b -> p (g b)").bitcast(FP8X4),
-                scales=a_scales[:, bt, passes, :].rearrange("p g b -> p (g b)"),
-                in_=grouped[:],
-            )
+            passes = slice(operand * GROUPS * P, (operand + 1) * GROUPS * P)
+            nc.vector.quantize_mx(out=a_codes[bt][:, passes].bitcast(FP8X4), scales=a_scales[bt][:, passes], in_=grouped[:])
 
         def quantise_chunk(chunk, x_copy_out):
             turned_x = [turn(x_sb, bt, x_copy_out) for bt in chunk]
@@ -165,13 +169,14 @@ def tile_slstmlayer_pa_kernel(
         def gate_products(gate, bt):
             banks = [psum_acc.tile([P, N_TILE], F32, name="acc%d" % nh, tag="acc") for nh in range(N_HALVES)]
             for ps in range(PASSES):
+                operand, g = divmod(ps, GROUPS)
                 for nh in range(N_HALVES):
                     nc.tensor.matmul_mx(
                         out=banks[nh][:],
-                        lhsT=a_codes[:, bt, ps, :].bitcast(FP8X4),
-                        lhsT_scale=a_scales[:, bt, ps, :],
-                        rhs=w_words[:, gate * PASSES + ps, 2 * nh * N_TILE : 2 * (nh + 1) * N_TILE].bitcast(FP4X4),
-                        rhs_scale=w_scales[:, gate * PASSES + ps, nh * N_TILE : (nh + 1) * N_TILE],
+                        lhsT=a_codes[bt][:, ps * P : (ps + 1) * P].bitcast(FP8X4),
+                        lhsT_scale=a_scales[bt][:, ps * P : (ps + 1) * P],
+                        rhs=w_words[gate][operand][:, g, 2 * nh * N_TILE : 2 * (nh + 1) * N_TILE].bitcast(FP4X4),
+                        rhs_scale=w_scales[gate][operand][:, g, nh * N_TILE : (nh + 1) * N_TILE],
                         start=(ps == 0),
                         stop=(ps == PASSES - 1),
                     )
@@ -183,18 +188,18 @@ def tile_slstmlayer_pa_kernel(
                 f_aff = work.tile([P, HIDDEN], F32)
                 for nh, cols in enumerate(halves):
                     nc.vector.tensor_tensor(out=f_aff[:, cols], in0=banks[nh][:], in1=bias_all[:, F_GATE, cols], op=ALU.add)
-                nc.scalar.activation(out=sig_f[:, bt, :], in_=f_aff[:], func=ACT.Sigmoid)
+                nc.scalar.activation(out=sig_f[bt][:], in_=f_aff[:], func=ACT.Sigmoid)
 
         def forget_paths(chunk):
             for bt in chunk:
                 log_s = work.tile([P, HIDDEN], F32)
-                nc.scalar.activation(out=log_s[:], in_=sig_f[:, bt, :], func=ACT.Ln, bias=ln_guard[:, 0:1])
+                nc.scalar.activation(out=log_s[:], in_=sig_f[bt][:], func=ACT.Ln, bias=ln_guard[:, 0:1])
                 for cols in halves:
                     nc.vector.scalar_tensor_tensor(
-                        out=f_path[:, bt, cols],
+                        out=f_path[bt][:, cols],
                         in0=log_s[:, cols],
                         scalar=LOG_FLOOR,
-                        in1=m_sb[:, bt, cols],
+                        in1=m_sb[bt][:, cols],
                         op0=ALU.max,
                         op1=ALU.add,
                     )
@@ -206,21 +211,21 @@ def tile_slstmlayer_pa_kernel(
             for nh, cols in enumerate(halves):
                 nc.vector.tensor_tensor(out=i_tilde[:, cols], in0=banks[nh][:], in1=bias_all[:, I_GATE, cols], op=ALU.add)
             for cols in halves:
-                nc.vector.tensor_tensor(out=diff[:, cols], in0=i_tilde[:, cols], in1=f_path[:, bt, cols], op=ALU.subtract)
+                nc.vector.tensor_tensor(out=diff[:, cols], in0=i_tilde[:, cols], in1=f_path[bt][:, cols], op=ALU.subtract)
             for cols in halves:
-                nc.vector.tensor_scalar_min(out=below[:, bt, cols], in0=diff[:, cols], scalar1=0.0)
+                nc.vector.tensor_scalar_min(out=below[bt][:, cols], in0=diff[:, cols], scalar1=0.0)
             for cols in halves:
-                nc.vector.tensor_scalar_max(out=above[:, bt, cols], in0=diff[:, cols], scalar1=0.0)
+                nc.vector.tensor_scalar_max(out=above[bt][:, cols], in0=diff[:, cols], scalar1=0.0)
             for cols in halves:
-                nc.vector.tensor_tensor(out=m_t[:, bt, cols], in0=i_tilde[:, cols], in1=f_path[:, bt, cols], op=ALU.max)
-            nc.sync.dma_start(out=out_0[bt * P : (bt + 1) * P, :], in_=m_t[:, bt, :])
+                nc.vector.tensor_tensor(out=m_t[bt][:, cols], in0=i_tilde[:, cols], in1=f_path[bt][:, cols], op=ALU.max)
+            nc.sync.dma_start(out=out_0[bt * P : (bt + 1) * P, :], in_=m_t[bt][:])
 
         def exponentials(bt):
             rows = slice(bt * P, (bt + 1) * P)
-            nc.scalar.activation(out=i_prime[:, bt, :], in_=below[:, bt, :], func=ACT.Exp)
-            nc.sync.dma_start(out=out_1[rows, :], in_=i_prime[:, bt, :])
-            nc.scalar.activation(out=f_prime[:, bt, :], in_=above[:, bt, :], func=ACT.Exp, scale=-1.0)
-            nc.sync.dma_start(out=out_2[rows, :], in_=f_prime[:, bt, :])
+            nc.scalar.activation(out=i_prime[bt][:], in_=below[bt][:], func=ACT.Exp)
+            nc.sync.dma_start(out=out_1[rows, :], in_=i_prime[bt][:])
+            nc.scalar.activation(out=f_prime[bt][:], in_=above[bt][:], func=ACT.Exp, scale=-1.0)
+            nc.sync.dma_start(out=out_2[rows, :], in_=f_prime[bt][:])
 
         forget_sigmoids(CHUNKS[0])
         quantise_chunk(CHUNKS[1], nc.vector.tensor_copy)

@@ -59,6 +59,7 @@ def tile_slstmlayer_pa_kernel(
         keep = ctx.enter_context(tc.tile_pool(name="keep", bufs=1))
         stage = ctx.enter_context(tc.tile_pool(name="stage", bufs=4))
         work = ctx.enter_context(tc.tile_pool(name="work", bufs=2))
+        outs = ctx.enter_context(tc.tile_pool(name="outs", bufs=3))
         psum_t = ctx.enter_context(tc.psum_pool(name="psum_t", bufs=2))
         psum_acc = ctx.enter_context(tc.psum_pool(name="psum_acc", bufs=6))
         ctx.enter_context(tc.manual_schedule())
@@ -85,12 +86,10 @@ def tile_slstmlayer_pa_kernel(
         ident = keep.tile([P, P], F32)
         ln_guard = keep.tile([P, 1], F32)
         sig_f = tiles_by_batch("sig_f", HIDDEN, F32)
-        f_path = tiles_by_batch("f_path", HIDDEN, F32)
+        m_rel = tiles_by_batch("m_rel", HIDDEN, F32)
+        f_rel = tiles_by_batch("f_rel", HIDDEN, F32)
         below = tiles_by_batch("below", HIDDEN, F32)
         above = tiles_by_batch("above", HIDDEN, F32)
-        m_t = tiles_by_batch("m_t", HIDDEN, F32)
-        i_prime = tiles_by_batch("i_prime", HIDDEN, F32)
-        f_prime = tiles_by_batch("f_prime", HIDDEN, F32)
 
         nc.vector.memset(bias_rows[:].rearrange("p g n -> p (g n)").bitcast(I32), 0)
         for gate in (F_GATE, I_GATE):
@@ -122,9 +121,9 @@ def tile_slstmlayer_pa_kernel(
         load_weight(F_GATE, 1, Wf_h_words, Wf_h_scales)
         load_rows(x_sb, x, CHUNKS[1])
         load_rows(h_sb, h_prev, CHUNKS[1])
+        load_rows(m_sb, m_prev, CHUNKS[0])
         load_weight(I_GATE, 0, Wi_x_words, Wi_x_scales)
         load_weight(I_GATE, 1, Wi_h_words, Wi_h_scales)
-        load_rows(m_sb, m_prev, CHUNKS[0])
         load_rows(m_sb, m_prev, CHUNKS[1])
 
         def turn(act_sb, bt, copy_out):
@@ -190,47 +189,55 @@ def tile_slstmlayer_pa_kernel(
                     nc.vector.tensor_tensor(out=f_aff[:, cols], in0=banks[nh][:], in1=bias_all[:, F_GATE, cols], op=ALU.add)
                 nc.scalar.activation(out=sig_f[bt][:], in_=f_aff[:], func=ACT.Sigmoid)
 
+        def relative_states(chunk):
+            for bt in chunk:
+                nc.gpsimd.tensor_tensor(out=m_rel[bt][:], in0=m_sb[bt][:], in1=bias_all[:, I_GATE, :], op=ALU.subtract)
+
         def forget_paths(chunk):
             for bt in chunk:
                 log_s = work.tile([P, HIDDEN], F32)
                 nc.scalar.activation(out=log_s[:], in_=sig_f[bt][:], func=ACT.Ln, bias=ln_guard[:, 0:1])
                 for cols in halves:
                     nc.vector.scalar_tensor_tensor(
-                        out=f_path[bt][:, cols],
+                        out=f_rel[bt][:, cols],
                         in0=log_s[:, cols],
                         scalar=LOG_FLOOR,
-                        in1=m_sb[bt][:, cols],
+                        in1=m_rel[bt][:, cols],
                         op0=ALU.max,
                         op1=ALU.add,
                     )
 
         def stabilise(bt):
             banks = gate_products(I_GATE, bt)
-            i_tilde = work.tile([P, HIDDEN], F32)
             diff = work.tile([P, HIDDEN], F32)
+            larger = work.tile([P, HIDDEN], F32)
+            m_t = outs.tile([P, HIDDEN], F32)
             for nh, cols in enumerate(halves):
-                nc.vector.tensor_tensor(out=i_tilde[:, cols], in0=banks[nh][:], in1=bias_all[:, I_GATE, cols], op=ALU.add)
-            for cols in halves:
-                nc.vector.tensor_tensor(out=diff[:, cols], in0=i_tilde[:, cols], in1=f_path[bt][:, cols], op=ALU.subtract)
+                nc.vector.tensor_tensor(out=diff[:, cols], in0=banks[nh][:], in1=f_rel[bt][:, cols], op=ALU.subtract)
+            for nh, cols in enumerate(halves):
+                nc.vector.tensor_tensor(out=larger[:, cols], in0=banks[nh][:], in1=f_rel[bt][:, cols], op=ALU.max)
             for cols in halves:
                 nc.vector.tensor_scalar_min(out=below[bt][:, cols], in0=diff[:, cols], scalar1=0.0)
             for cols in halves:
                 nc.vector.tensor_scalar_max(out=above[bt][:, cols], in0=diff[:, cols], scalar1=0.0)
-            for cols in halves:
-                nc.vector.tensor_tensor(out=m_t[bt][:, cols], in0=i_tilde[:, cols], in1=f_path[bt][:, cols], op=ALU.max)
-            nc.sync.dma_start(out=out_0[bt * P : (bt + 1) * P, :], in_=m_t[bt][:])
+            nc.gpsimd.tensor_tensor(out=m_t[:], in0=larger[:], in1=bias_all[:, I_GATE, :], op=ALU.add)
+            nc.sync.dma_start(out=out_0[bt * P : (bt + 1) * P, :], in_=m_t[:])
 
         def exponentials(bt):
             rows = slice(bt * P, (bt + 1) * P)
-            nc.scalar.activation(out=i_prime[bt][:], in_=below[bt][:], func=ACT.Exp)
-            nc.sync.dma_start(out=out_1[rows, :], in_=i_prime[bt][:])
-            nc.scalar.activation(out=f_prime[bt][:], in_=above[bt][:], func=ACT.Exp, scale=-1.0)
-            nc.sync.dma_start(out=out_2[rows, :], in_=f_prime[bt][:])
+            i_prime = outs.tile([P, HIDDEN], F32)
+            nc.scalar.activation(out=i_prime[:], in_=below[bt][:], func=ACT.Exp)
+            nc.sync.dma_start(out=out_1[rows, :], in_=i_prime[:])
+            f_prime = outs.tile([P, HIDDEN], F32)
+            nc.scalar.activation(out=f_prime[:], in_=above[bt][:], func=ACT.Exp, scale=-1.0)
+            nc.sync.dma_start(out=out_2[rows, :], in_=f_prime[:])
 
         forget_sigmoids(CHUNKS[0])
         quantise_chunk(CHUNKS[1], nc.vector.tensor_copy)
+        relative_states(CHUNKS[0])
         forget_paths(CHUNKS[0])
         forget_sigmoids(CHUNKS[1])
+        relative_states(CHUNKS[1])
         for bt in CHUNKS[0]:
             stabilise(bt)
         forget_paths(CHUNKS[1])

@@ -59,7 +59,6 @@ def tile_slstmlayer_pa_kernel(
         keep = ctx.enter_context(tc.tile_pool(name="keep", bufs=1))
         stage = ctx.enter_context(tc.tile_pool(name="stage", bufs=4))
         work = ctx.enter_context(tc.tile_pool(name="work", bufs=2))
-        outs = ctx.enter_context(tc.tile_pool(name="outs", bufs=3))
         psum_t = ctx.enter_context(tc.psum_pool(name="psum_t", bufs=2))
         psum_acc = ctx.enter_context(tc.psum_pool(name="psum_acc", bufs=6))
         ctx.enter_context(tc.manual_schedule())
@@ -86,10 +85,12 @@ def tile_slstmlayer_pa_kernel(
         ident = keep.tile([P, P], F32)
         ln_guard = keep.tile([P, 1], F32)
         sig_f = tiles_by_batch("sig_f", HIDDEN, F32)
-        m_rel = tiles_by_batch("m_rel", HIDDEN, F32)
-        f_rel = tiles_by_batch("f_rel", HIDDEN, F32)
+        f_path = tiles_by_batch("f_path", HIDDEN, F32)
         below = tiles_by_batch("below", HIDDEN, F32)
         above = tiles_by_batch("above", HIDDEN, F32)
+        m_t = tiles_by_batch("m_t", HIDDEN, F32)
+        i_prime = tiles_by_batch("i_prime", HIDDEN, F32)
+        f_prime = tiles_by_batch("f_prime", HIDDEN, F32)
 
         nc.vector.memset(bias_rows[:].rearrange("p g n -> p (g n)").bitcast(I32), 0)
         for gate in (F_GATE, I_GATE):
@@ -99,9 +100,8 @@ def tile_slstmlayer_pa_kernel(
         nc.vector.memset(ln_guard[:], LN_GUARD)
         make_identity(nc, ident[:])
 
-        def load_rows(tiles_sb, source, chunk):
-            for bt in chunk:
-                nc.sync.dma_start(out=tiles_sb[bt][:], in_=source[bt * P : (bt + 1) * P, :])
+        def load_rows(tiles_sb, source, bt):
+            nc.sync.dma_start(out=tiles_sb[bt][:], in_=source[bt * P : (bt + 1) * P, :])
 
         def load_weight(gate, operand, words, scales):
             for r in range(4):
@@ -113,18 +113,20 @@ def tile_slstmlayer_pa_kernel(
                 out=w_words[gate][operand][:].bitcast(I32), in_=words.rearrange("g p c -> p g c").bitcast(I32)
             )
 
-        load_rows(x_sb, x, CHUNKS[0])
-        load_rows(h_sb, h_prev, CHUNKS[0])
+        for bt in CHUNKS[0]:
+            load_rows(x_sb, x, bt)
+            load_rows(h_sb, h_prev, bt)
         nc.sync.dma_start(out=bias_rows[0:1, F_GATE, :], in_=b_f.rearrange("(o n) -> o n", o=1))
         nc.sync.dma_start(out=bias_rows[0:1, I_GATE, :], in_=b_i.rearrange("(o n) -> o n", o=1))
         load_weight(F_GATE, 0, Wf_x_words, Wf_x_scales)
         load_weight(F_GATE, 1, Wf_h_words, Wf_h_scales)
-        load_rows(x_sb, x, CHUNKS[1])
-        load_rows(h_sb, h_prev, CHUNKS[1])
-        load_rows(m_sb, m_prev, CHUNKS[0])
+        for bt in CHUNKS[1]:
+            load_rows(x_sb, x, bt)
+            load_rows(h_sb, h_prev, bt)
         load_weight(I_GATE, 0, Wi_x_words, Wi_x_scales)
         load_weight(I_GATE, 1, Wi_h_words, Wi_h_scales)
-        load_rows(m_sb, m_prev, CHUNKS[1])
+        for bt in range(BATCH_TILES):
+            load_rows(m_sb, m_prev, bt)
 
         def turn(act_sb, bt, copy_out):
             row_words = act_sb[bt][:].bitcast(F32)
@@ -148,22 +150,24 @@ def tile_slstmlayer_pa_kernel(
             nc.vector.quantize_mx(out=a_codes[bt][:, passes].bitcast(FP8X4), scales=a_scales[bt][:, passes], in_=grouped[:])
 
         def quantise_chunk(chunk, x_copy_out):
-            turned_x = [turn(x_sb, bt, x_copy_out) for bt in chunk]
-            turned_h = [turn(h_sb, bt, nc.vector.tensor_copy) for bt in chunk]
-            for j, bt in enumerate(chunk):
-                quantise(turned_x[j], bt, 0)
-                quantise(turned_h[j], bt, 1)
+            for bt in chunk:
+                grouped_x = turn(x_sb, bt, x_copy_out)
+                grouped_h = turn(h_sb, bt, nc.vector.tensor_copy)
+                quantise(grouped_x, bt, 0)
+                quantise(grouped_h, bt, 1)
 
         quantise_chunk(CHUNKS[0], nc.scalar.copy)
 
-        for gate in (F_GATE, I_GATE):
-            for nh in range(N_HALVES):
-                cols = slice(nh * N_TILE, (nh + 1) * N_TILE)
+        halves = [slice(nh * N_TILE, (nh + 1) * N_TILE) for nh in range(N_HALVES)]
+        whole = [slice(0, HIDDEN)]
+
+        def spread_bias(gate):
+            for cols in halves:
                 spread = psum_acc.tile([P, N_TILE], F32, tag="acc")
                 nc.tensor.matmul(out=spread[:], lhsT=ones[:], rhs=bias_rows[:, gate, cols], start=True, stop=True)
                 nc.scalar.copy(out=bias_all[:, gate, cols], in_=spread[:])
 
-        halves = [slice(nh * N_TILE, (nh + 1) * N_TILE) for nh in range(N_HALVES)]
+        spread_bias(F_GATE)
 
         def gate_products(gate, bt):
             banks = [psum_acc.tile([P, N_TILE], F32, name="acc%d" % nh, tag="acc") for nh in range(N_HALVES)]
@@ -189,60 +193,61 @@ def tile_slstmlayer_pa_kernel(
                     nc.vector.tensor_tensor(out=f_aff[:, cols], in0=banks[nh][:], in1=bias_all[:, F_GATE, cols], op=ALU.add)
                 nc.scalar.activation(out=sig_f[bt][:], in_=f_aff[:], func=ACT.Sigmoid)
 
-        def relative_states(chunk):
-            for bt in chunk:
-                nc.gpsimd.tensor_tensor(out=m_rel[bt][:], in0=m_sb[bt][:], in1=bias_all[:, I_GATE, :], op=ALU.subtract)
-
         def forget_paths(chunk):
             for bt in chunk:
                 log_s = work.tile([P, HIDDEN], F32)
                 nc.scalar.activation(out=log_s[:], in_=sig_f[bt][:], func=ACT.Ln, bias=ln_guard[:, 0:1])
                 for cols in halves:
                     nc.vector.scalar_tensor_tensor(
-                        out=f_rel[bt][:, cols],
+                        out=f_path[bt][:, cols],
                         in0=log_s[:, cols],
                         scalar=LOG_FLOOR,
-                        in1=m_rel[bt][:, cols],
+                        in1=m_sb[bt][:, cols],
                         op0=ALU.max,
                         op1=ALU.add,
                     )
 
-        def stabilise(bt):
+        def stabilise(bt, pieces, above_engine):
             banks = gate_products(I_GATE, bt)
+            i_tilde = work.tile([P, HIDDEN], F32)
             diff = work.tile([P, HIDDEN], F32)
-            larger = work.tile([P, HIDDEN], F32)
-            m_t = outs.tile([P, HIDDEN], F32)
             for nh, cols in enumerate(halves):
-                nc.vector.tensor_tensor(out=diff[:, cols], in0=banks[nh][:], in1=f_rel[bt][:, cols], op=ALU.subtract)
-            for nh, cols in enumerate(halves):
-                nc.vector.tensor_tensor(out=larger[:, cols], in0=banks[nh][:], in1=f_rel[bt][:, cols], op=ALU.max)
+                nc.vector.tensor_tensor(out=i_tilde[:, cols], in0=banks[nh][:], in1=bias_all[:, I_GATE, cols], op=ALU.add)
+            for cols in halves:
+                nc.vector.tensor_tensor(out=diff[:, cols], in0=i_tilde[:, cols], in1=f_path[bt][:, cols], op=ALU.subtract)
             for cols in halves:
                 nc.vector.tensor_scalar_min(out=below[bt][:, cols], in0=diff[:, cols], scalar1=0.0)
+            if above_engine == "vector":
+                for cols in halves:
+                    nc.vector.tensor_scalar_max(out=above[bt][:, cols], in0=diff[:, cols], scalar1=0.0)
+            else:
+                for cols in pieces:
+                    nc.scalar.activation(out=above[bt][:, cols], in_=diff[:, cols], func=ACT.Relu)
             for cols in halves:
-                nc.vector.tensor_scalar_max(out=above[bt][:, cols], in0=diff[:, cols], scalar1=0.0)
-            nc.gpsimd.tensor_tensor(out=m_t[:], in0=larger[:], in1=bias_all[:, I_GATE, :], op=ALU.add)
-            nc.sync.dma_start(out=out_0[bt * P : (bt + 1) * P, :], in_=m_t[:])
+                nc.vector.tensor_tensor(out=m_t[bt][:, cols], in0=i_tilde[:, cols], in1=f_path[bt][:, cols], op=ALU.max)
+            for cols in pieces:
+                nc.sync.dma_start(out=out_0[bt * P : (bt + 1) * P, cols], in_=m_t[bt][:, cols])
 
-        def exponentials(bt):
+        def exponentials(bt, pieces):
             rows = slice(bt * P, (bt + 1) * P)
-            i_prime = outs.tile([P, HIDDEN], F32)
-            nc.scalar.activation(out=i_prime[:], in_=below[bt][:], func=ACT.Exp)
-            nc.sync.dma_start(out=out_1[rows, :], in_=i_prime[:])
-            f_prime = outs.tile([P, HIDDEN], F32)
-            nc.scalar.activation(out=f_prime[:], in_=above[bt][:], func=ACT.Exp, scale=-1.0)
-            nc.sync.dma_start(out=out_2[rows, :], in_=f_prime[:])
+            for cols in pieces:
+                nc.scalar.activation(out=i_prime[bt][:, cols], in_=below[bt][:, cols], func=ACT.Exp)
+                nc.sync.dma_start(out=out_1[rows, cols], in_=i_prime[bt][:, cols])
+            for cols in pieces:
+                nc.scalar.activation(out=f_prime[bt][:, cols], in_=above[bt][:, cols], func=ACT.Exp, scale=-1.0)
+                nc.sync.dma_start(out=out_2[rows, cols], in_=f_prime[bt][:, cols])
 
         forget_sigmoids(CHUNKS[0])
+        spread_bias(I_GATE)
         quantise_chunk(CHUNKS[1], nc.vector.tensor_copy)
-        relative_states(CHUNKS[0])
         forget_paths(CHUNKS[0])
         forget_sigmoids(CHUNKS[1])
-        relative_states(CHUNKS[1])
         for bt in CHUNKS[0]:
-            stabilise(bt)
+            stabilise(bt, whole, "vector")
         forget_paths(CHUNKS[1])
         for bt in CHUNKS[0]:
-            exponentials(bt)
+            exponentials(bt, whole)
         for bt in CHUNKS[1]:
-            stabilise(bt)
-            exponentials(bt)
+            pieces = halves if bt == BATCH_TILES - 1 else whole
+            stabilise(bt, pieces, "scalar")
+            exponentials(bt, pieces)

@@ -79,8 +79,9 @@ def tile_slstmlayer_pa_kernel(
         ]
         a_codes = tiles_by_batch("a_codes", PASSES * P, U32)
         a_scales = tiles_by_batch("a_scales", PASSES * P, U8)
-        bias_rows = keep.tile([P, 2, HIDDEN], BF16)
-        bias_all = keep.tile([P, 2, HIDDEN], F32)
+        bias_rows = keep.tile([P, HIDDEN], BF16)
+        bias_f_all = keep.tile([P, HIDDEN], F32)
+        bias_i_all = keep.tile([P, HIDDEN], BF16)
         ones = keep.tile([P, P], BF16)
         ident = keep.tile([P, P], F32)
         ln_guard = keep.tile([P, 1], F32)
@@ -92,7 +93,7 @@ def tile_slstmlayer_pa_kernel(
         i_prime = tiles_by_batch("i_prime", HIDDEN, F32)
         f_prime = tiles_by_batch("f_prime", HIDDEN, F32)
 
-        nc.vector.memset(bias_rows[:].rearrange("p g n -> p (g n)").bitcast(I32), 0)
+        nc.vector.memset(bias_rows[:].bitcast(I32), 0)
         for gate in (F_GATE, I_GATE):
             for planes in w_scales[gate]:
                 nc.vector.memset(planes[:].rearrange("p s n -> p (s n)").bitcast(I32), 0)
@@ -116,8 +117,7 @@ def tile_slstmlayer_pa_kernel(
         for bt in CHUNKS[0]:
             load_rows(x_sb, x, bt)
             load_rows(h_sb, h_prev, bt)
-        nc.sync.dma_start(out=bias_rows[0:1, F_GATE, :], in_=b_f.rearrange("(o n) -> o n", o=1))
-        nc.sync.dma_start(out=bias_rows[0:1, I_GATE, :], in_=b_i.rearrange("(o n) -> o n", o=1))
+        nc.sync.dma_start(out=bias_rows[0:1, :], in_=b_f.rearrange("(o n) -> o n", o=1))
         load_weight(F_GATE, 0, Wf_x_words, Wf_x_scales)
         load_weight(F_GATE, 1, Wf_h_words, Wf_h_scales)
         for bt in CHUNKS[1]:
@@ -127,6 +127,7 @@ def tile_slstmlayer_pa_kernel(
         load_weight(I_GATE, 1, Wi_h_words, Wi_h_scales)
         for bt in range(BATCH_TILES):
             load_rows(m_sb, m_prev, bt)
+        nc.sync.dma_start(out=bias_i_all[:], in_=b_i.partition_broadcast(P))
 
         def turn(act_sb, bt, copy_out):
             row_words = act_sb[bt][:].bitcast(F32)
@@ -161,13 +162,10 @@ def tile_slstmlayer_pa_kernel(
         halves = [slice(nh * N_TILE, (nh + 1) * N_TILE) for nh in range(N_HALVES)]
         whole = [slice(0, HIDDEN)]
 
-        def spread_bias(gate):
-            for cols in halves:
-                spread = psum_acc.tile([P, N_TILE], F32, tag="acc")
-                nc.tensor.matmul(out=spread[:], lhsT=ones[:], rhs=bias_rows[:, gate, cols], start=True, stop=True)
-                nc.scalar.copy(out=bias_all[:, gate, cols], in_=spread[:])
-
-        spread_bias(F_GATE)
+        for cols in halves:
+            spread = psum_acc.tile([P, N_TILE], F32, tag="acc")
+            nc.tensor.matmul(out=spread[:], lhsT=ones[:], rhs=bias_rows[:, cols], start=True, stop=True)
+            nc.scalar.copy(out=bias_f_all[:, cols], in_=spread[:])
 
         def gate_products(gate, bt):
             banks = [psum_acc.tile([P, N_TILE], F32, name="acc%d" % nh, tag="acc") for nh in range(N_HALVES)]
@@ -190,7 +188,7 @@ def tile_slstmlayer_pa_kernel(
                 banks = gate_products(F_GATE, bt)
                 f_aff = work.tile([P, HIDDEN], F32)
                 for nh, cols in enumerate(halves):
-                    nc.vector.tensor_tensor(out=f_aff[:, cols], in0=banks[nh][:], in1=bias_all[:, F_GATE, cols], op=ALU.add)
+                    nc.vector.tensor_tensor(out=f_aff[:, cols], in0=banks[nh][:], in1=bias_f_all[:, cols], op=ALU.add)
                 nc.scalar.activation(out=sig_f[bt][:], in_=f_aff[:], func=ACT.Sigmoid)
 
         def forget_paths(chunk):
@@ -207,12 +205,17 @@ def tile_slstmlayer_pa_kernel(
                         op1=ALU.add,
                     )
 
-        def stabilise(bt, pieces, above_engine):
+        def stabilise(bt, pieces, above_engine, m_t_first):
             banks = gate_products(I_GATE, bt)
             i_tilde = work.tile([P, HIDDEN], F32)
             diff = work.tile([P, HIDDEN], F32)
             for nh, cols in enumerate(halves):
-                nc.vector.tensor_tensor(out=i_tilde[:, cols], in0=banks[nh][:], in1=bias_all[:, I_GATE, cols], op=ALU.add)
+                nc.vector.tensor_tensor(out=i_tilde[:, cols], in0=banks[nh][:], in1=bias_i_all[:, cols], op=ALU.add)
+            if m_t_first:
+                for cols in halves:
+                    nc.vector.tensor_tensor(out=m_t[bt][:, cols], in0=i_tilde[:, cols], in1=f_path[bt][:, cols], op=ALU.max)
+                for cols in pieces:
+                    nc.sync.dma_start(out=out_0[bt * P : (bt + 1) * P, cols], in_=m_t[bt][:, cols])
             for cols in halves:
                 nc.vector.tensor_tensor(out=diff[:, cols], in0=i_tilde[:, cols], in1=f_path[bt][:, cols], op=ALU.subtract)
             for cols in halves:
@@ -223,10 +226,11 @@ def tile_slstmlayer_pa_kernel(
             else:
                 for cols in pieces:
                     nc.scalar.activation(out=above[bt][:, cols], in_=diff[:, cols], func=ACT.Relu)
-            for cols in halves:
-                nc.vector.tensor_tensor(out=m_t[bt][:, cols], in0=i_tilde[:, cols], in1=f_path[bt][:, cols], op=ALU.max)
-            for cols in pieces:
-                nc.sync.dma_start(out=out_0[bt * P : (bt + 1) * P, cols], in_=m_t[bt][:, cols])
+            if not m_t_first:
+                for cols in halves:
+                    nc.vector.tensor_tensor(out=m_t[bt][:, cols], in0=i_tilde[:, cols], in1=f_path[bt][:, cols], op=ALU.max)
+                for cols in pieces:
+                    nc.sync.dma_start(out=out_0[bt * P : (bt + 1) * P, cols], in_=m_t[bt][:, cols])
 
         def exponentials(bt, pieces):
             rows = slice(bt * P, (bt + 1) * P)
@@ -238,16 +242,15 @@ def tile_slstmlayer_pa_kernel(
                 nc.sync.dma_start(out=out_2[rows, cols], in_=f_prime[bt][:, cols])
 
         forget_sigmoids(CHUNKS[0])
-        spread_bias(I_GATE)
         quantise_chunk(CHUNKS[1], nc.vector.tensor_copy)
         forget_paths(CHUNKS[0])
         forget_sigmoids(CHUNKS[1])
         for bt in CHUNKS[0]:
-            stabilise(bt, whole, "vector")
+            stabilise(bt, whole, "vector", True)
         forget_paths(CHUNKS[1])
         for bt in CHUNKS[0]:
             exponentials(bt, whole)
         for bt in CHUNKS[1]:
             pieces = halves if bt == BATCH_TILES - 1 else whole
-            stabilise(bt, pieces, "scalar")
+            stabilise(bt, pieces, "scalar", False)
             exponentials(bt, pieces)

@@ -90,6 +90,7 @@ def tile_slstmlayer_pa_kernel(
         below = tiles_by_batch("below", HIDDEN, F32)
         above = tiles_by_batch("above", HIDDEN, F32)
         m_t = tiles_by_batch("m_t", HIDDEN, F32)
+        diffs = tiles_by_batch("diffs", HIDDEN, F32)
         i_prime = tiles_by_batch("i_prime", HIDDEN, F32)
         f_prime = tiles_by_batch("f_prime", HIDDEN, F32)
 
@@ -208,7 +209,7 @@ def tile_slstmlayer_pa_kernel(
         def stabilise(bt, pieces, above_engine, m_t_first):
             banks = gate_products(I_GATE, bt)
             i_tilde = work.tile([P, HIDDEN], F32)
-            diff = work.tile([P, HIDDEN], F32)
+            diff = diffs[bt]
             for nh, cols in enumerate(halves):
                 nc.vector.tensor_tensor(out=i_tilde[:, cols], in0=banks[nh][:], in1=bias_i_all[:, cols], op=ALU.add)
             if m_t_first:
@@ -223,7 +224,7 @@ def tile_slstmlayer_pa_kernel(
             if above_engine == "vector":
                 for cols in halves:
                     nc.vector.tensor_scalar_max(out=above[bt][:, cols], in0=diff[:, cols], scalar1=0.0)
-            else:
+            elif above_engine == "scalar":
                 for cols in pieces:
                     nc.scalar.activation(out=above[bt][:, cols], in_=diff[:, cols], func=ACT.Relu)
             if not m_t_first:
@@ -232,8 +233,10 @@ def tile_slstmlayer_pa_kernel(
                 for cols in pieces:
                     nc.sync.dma_start(out=out_0[bt * P : (bt + 1) * P, cols], in_=m_t[bt][:, cols])
 
-        def exponentials(bt, pieces):
+        def exponentials(bt, pieces, relu_first=False):
             rows = slice(bt * P, (bt + 1) * P)
+            if relu_first:
+                nc.scalar.activation(out=above[bt][:], in_=diffs[bt][:], func=ACT.Relu)
             for cols in pieces:
                 nc.scalar.activation(out=i_prime[bt][:, cols], in_=below[bt][:, cols], func=ACT.Exp)
                 nc.sync.dma_start(out=out_1[rows, cols], in_=i_prime[bt][:, cols])
@@ -246,10 +249,10 @@ def tile_slstmlayer_pa_kernel(
         forget_paths(CHUNKS[0])
         forget_sigmoids(CHUNKS[1])
         for bt in CHUNKS[0]:
-            stabilise(bt, whole, "vector", True)
+            stabilise(bt, whole, "vector" if bt == 0 else "later", True)
         forget_paths(CHUNKS[1])
         for bt in CHUNKS[0]:
-            exponentials(bt, whole)
+            exponentials(bt, whole, relu_first=(bt == 1))
         for bt in CHUNKS[1]:
             pieces = halves if bt == BATCH_TILES - 1 else whole
             stabilise(bt, pieces, "scalar", False)

@@ -83,6 +83,7 @@ def tile_slstmlayer_pa_kernel(
         bias_f_all = keep.tile([P, HIDDEN], F32)
         bias_i_all = keep.tile([P, HIDDEN], BF16)
         ones = keep.tile([P, P], BF16)
+        idle_rhs = keep.tile([P, N_TILE], BF16)
         ident = keep.tile([P, P], F32)
         ln_guard = keep.tile([P, 1], F32)
         sig_f = tiles_by_batch("sig_f", HIDDEN, F32)
@@ -94,11 +95,12 @@ def tile_slstmlayer_pa_kernel(
         i_prime = tiles_by_batch("i_prime", HIDDEN, F32)
         f_prime = tiles_by_batch("f_prime", HIDDEN, F32)
 
+        nc.vector.memset(ones[:], 1.0)
+        nc.vector.memset(idle_rhs[:], 0.0)
         nc.vector.memset(bias_rows[:].bitcast(I32), 0)
         for gate in (F_GATE, I_GATE):
             for planes in w_scales[gate]:
                 nc.vector.memset(planes[:].rearrange("p s n -> p (s n)").bitcast(I32), 0)
-        nc.vector.memset(ones[:], 1.0)
         nc.vector.memset(ln_guard[:], LN_GUARD)
         make_identity(nc, ident[:])
 
@@ -130,6 +132,13 @@ def tile_slstmlayer_pa_kernel(
             load_rows(m_sb, m_prev, bt)
         nc.sync.dma_start(out=bias_i_all[:], in_=b_i.partition_broadcast(P))
 
+        def keep_clock(count):
+            unread = psum_acc.tile([P, N_TILE], F32, tag="acc")
+            for step in range(count):
+                nc.tensor.matmul(out=unread[:], lhsT=ones[:], rhs=idle_rhs[:], start=True, stop=True)
+
+        keep_clock(4)
+
         def turn(act_sb, bt, copy_out):
             row_words = act_sb[bt][:].bitcast(F32)
             turned = psum_t.tile([P, GROUPS, 2, P], F32)
@@ -155,6 +164,7 @@ def tile_slstmlayer_pa_kernel(
             for bt in chunk:
                 grouped_x = turn(x_sb, bt, x_copy_out)
                 grouped_h = turn(h_sb, bt, nc.vector.tensor_copy)
+                keep_clock(2)
                 quantise(grouped_x, bt, 0)
                 quantise(grouped_h, bt, 1)
 
@@ -192,19 +202,21 @@ def tile_slstmlayer_pa_kernel(
                     nc.vector.tensor_tensor(out=f_aff[:, cols], in0=banks[nh][:], in1=bias_f_all[:, cols], op=ALU.add)
                 nc.scalar.activation(out=sig_f[bt][:], in_=f_aff[:], func=ACT.Sigmoid)
 
-        def forget_paths(chunk):
-            for bt in chunk:
-                log_s = work.tile([P, HIDDEN], F32)
-                nc.scalar.activation(out=log_s[:], in_=sig_f[bt][:], func=ACT.Ln, bias=ln_guard[:, 0:1])
-                for cols in halves:
-                    nc.vector.scalar_tensor_tensor(
-                        out=f_path[bt][:, cols],
-                        in0=log_s[:, cols],
-                        scalar=LOG_FLOOR,
-                        in1=m_sb[bt][:, cols],
-                        op0=ALU.max,
-                        op1=ALU.add,
-                    )
+        def logarithm(bt):
+            log_s = work.tile([P, HIDDEN], F32)
+            nc.scalar.activation(out=log_s[:], in_=sig_f[bt][:], func=ACT.Ln, bias=ln_guard[:, 0:1])
+            return log_s
+
+        def forget_path(bt, log_s):
+            for cols in whole:
+                nc.vector.scalar_tensor_tensor(
+                    out=f_path[bt][:, cols],
+                    in0=log_s[:, cols],
+                    scalar=LOG_FLOOR,
+                    in1=m_sb[bt][:, cols],
+                    op0=ALU.max,
+                    op1=ALU.add,
+                )
 
         def stabilise(bt, pieces, above_engine, m_t_first):
             banks = gate_products(I_GATE, bt)
@@ -230,8 +242,28 @@ def tile_slstmlayer_pa_kernel(
             if not m_t_first:
                 for cols in halves:
                     nc.vector.tensor_tensor(out=m_t[bt][:, cols], in0=i_tilde[:, cols], in1=f_path[bt][:, cols], op=ALU.max)
-                for cols in pieces:
-                    nc.sync.dma_start(out=out_0[bt * P : (bt + 1) * P, cols], in_=m_t[bt][:, cols])
+                if bt != BATCH_TILES - 1:
+                    for cols in pieces:
+                        nc.sync.dma_start(out=out_0[bt * P : (bt + 1) * P, cols], in_=m_t[bt][:, cols])
+
+        def stabilise_pair(bt_a, bt_b, fillers):
+            tildes = {}
+
+            def products_and_max(bt):
+                banks = gate_products(I_GATE, bt)
+                i_tilde = work.tile([P, HIDDEN], F32)
+                tildes[bt] = i_tilde
+                for nh, cols in enumerate(halves):
+                    nc.vector.tensor_tensor(out=i_tilde[:, cols], in0=banks[nh][:], in1=bias_i_all[:, cols], op=ALU.add)
+                for cols in halves:
+                    nc.vector.tensor_tensor(out=m_t[bt][:, cols], in0=i_tilde[:, cols], in1=f_path[bt][:, cols], op=ALU.max)
+                nc.sync.dma_start(out=out_0[bt * P : (bt + 1) * P, :], in_=m_t[bt][:])
+                nc.vector.tensor_tensor(out=diffs[bt][:], in0=i_tilde[:], in1=f_path[bt][:], op=ALU.subtract)
+
+            products_and_max(bt_a)
+            products_and_max(bt_b)
+            nc.vector.tensor_scalar_min(out=below[bt_a][:], in0=diffs[bt_a][:], scalar1=0.0)
+            nc.vector.tensor_scalar_min(out=below[bt_b][:], in0=diffs[bt_b][:], scalar1=0.0)
 
         def exponentials(bt, pieces, relu_first=False):
             rows = slice(bt * P, (bt + 1) * P)
@@ -240,20 +272,25 @@ def tile_slstmlayer_pa_kernel(
             for cols in pieces:
                 nc.scalar.activation(out=i_prime[bt][:, cols], in_=below[bt][:, cols], func=ACT.Exp)
                 nc.sync.dma_start(out=out_1[rows, cols], in_=i_prime[bt][:, cols])
+            if bt == BATCH_TILES - 1:
+                for cols in pieces:
+                    nc.sync.dma_start(out=out_0[rows, cols], in_=m_t[bt][:, cols])
             for cols in pieces:
                 nc.scalar.activation(out=f_prime[bt][:, cols], in_=above[bt][:, cols], func=ACT.Exp, scale=-1.0)
                 nc.sync.dma_start(out=out_2[rows, cols], in_=f_prime[bt][:, cols])
 
         forget_sigmoids(CHUNKS[0])
         quantise_chunk(CHUNKS[1], nc.vector.tensor_copy)
-        forget_paths(CHUNKS[0])
-        forget_sigmoids(CHUNKS[1])
+        first_logs = [logarithm(bt) for bt in CHUNKS[0]]
+        for bt_first, bt_second, log_s in zip(CHUNKS[0], CHUNKS[1], first_logs):
+            forget_sigmoids((bt_second,))
+            forget_path(bt_first, log_s)
+        stabilise_pair(CHUNKS[0][0], CHUNKS[0][1], ())
+        for bt in CHUNKS[1]:
+            forget_path(bt, logarithm(bt))
         for bt in CHUNKS[0]:
-            stabilise(bt, whole, "vector" if bt == 0 else "later", True)
-        forget_paths(CHUNKS[1])
-        for bt in CHUNKS[0]:
-            exponentials(bt, whole, relu_first=(bt == 1))
+            exponentials(bt, whole, relu_first=True)
         for bt in CHUNKS[1]:
             pieces = halves if bt == BATCH_TILES - 1 else whole
-            stabilise(bt, pieces, "scalar", False)
+            stabilise(bt, pieces, "vector" if bt == BATCH_TILES - 1 else "scalar", False)
             exponentials(bt, pieces)

@@ -20,13 +20,14 @@ FEATURES = 1024
 HIDDEN = 1024
 K_PASS = 4 * P
 BATCH_TILES = BATCH // P
+HIDDEN_TILES = HIDDEN // P
 GROUPS = FEATURES // K_PASS
 PASSES = 2 * GROUPS
 N_TILE = 512
 N_HALVES = HIDDEN // N_TILE
+TILES_PER_BANK = N_TILE // P
 WORDS_PER_GROUP = K_PASS // 2
 F_GATE, I_GATE = 0, 1
-CHUNKS = ((0, 1), (2, 3))
 
 SIGMOID_FLOOR = 1e-8
 LOG_FLOOR = math.log(SIGMOID_FLOOR)
@@ -58,17 +59,22 @@ def tile_slstmlayer_pa_kernel(
     with ExitStack() as ctx:
         keep = ctx.enter_context(tc.tile_pool(name="keep", bufs=1))
         stage = ctx.enter_context(tc.tile_pool(name="stage", bufs=4))
-        work = ctx.enter_context(tc.tile_pool(name="work", bufs=2))
-        psum_t = ctx.enter_context(tc.psum_pool(name="psum_t", bufs=2))
         psum_acc = ctx.enter_context(tc.psum_pool(name="psum_acc", bufs=6))
+        psum_side = ctx.enter_context(tc.psum_pool(name="psum_side", bufs=2))
         ctx.enter_context(tc.manual_schedule())
 
-        def tiles_by_batch(name, width, dtype):
-            return [keep.tile([P, width], dtype, name="%s%d" % (name, bt), align_bytes=64) for bt in range(BATCH_TILES)]
+        def acc_bank(name):
+            return psum_acc.tile([P, N_TILE], F32, name=name, tag="acc")
 
-        x_sb = tiles_by_batch("x_sb", FEATURES, BF16)
-        h_sb = tiles_by_batch("h_sb", FEATURES, BF16)
-        m_sb = tiles_by_batch("m_sb", HIDDEN, BF16)
+        def side_bank(name):
+            return psum_side.tile([P, N_TILE], F32, name=name, tag="side")
+
+        def tiles(name, count, width, dtype):
+            return [keep.tile([P, width], dtype, name="%s%d" % (name, j), align_bytes=64) for j in range(count)]
+
+        x_sb = tiles("x_sb", BATCH_TILES, FEATURES, BF16)
+        h_sb = tiles("h_sb", BATCH_TILES, FEATURES, BF16)
+        m_sb = tiles("m_sb", BATCH_TILES, HIDDEN, BF16)
         w_words = [
             [keep.tile([P, GROUPS, 2 * HIDDEN], U8, name="w_words%d%d" % (gate, o), align_bytes=64) for o in range(2)]
             for gate in range(2)
@@ -77,220 +83,377 @@ def tile_slstmlayer_pa_kernel(
             [keep.tile([P, GROUPS, HIDDEN], U8, name="w_scales%d%d" % (gate, o), align_bytes=64) for o in range(2)]
             for gate in range(2)
         ]
-        a_codes = tiles_by_batch("a_codes", PASSES * P, U32)
-        a_scales = tiles_by_batch("a_scales", PASSES * P, U8)
-        bias_rows = keep.tile([P, HIDDEN], BF16)
-        bias_f_all = keep.tile([P, HIDDEN], F32)
-        bias_i_all = keep.tile([P, HIDDEN], BF16)
+        a_codes = tiles("a_codes", PASSES, BATCH, U32)
+        a_scales = tiles("a_scales", PASSES, BATCH, U8)
+        bias_rows_f = keep.tile([P, P], BF16)
+        bias_rows_i = keep.tile([P, HIDDEN], BF16)
+        bias_f = keep.tile([P, HIDDEN_TILES], F32)
+        bias_i = keep.tile([P, HIDDEN], F32)
         ones = keep.tile([P, P], BF16)
         idle_rhs = keep.tile([P, N_TILE], BF16)
         ident = keep.tile([P, P], F32)
+        ident_head = keep.tile([P, HIDDEN_TILES], BF16)
         ln_guard = keep.tile([P, 1], F32)
-        sig_f = tiles_by_batch("sig_f", HIDDEN, F32)
-        f_path = tiles_by_batch("f_path", HIDDEN, F32)
-        below = tiles_by_batch("below", HIDDEN, F32)
-        above = tiles_by_batch("above", HIDDEN, F32)
-        m_t = tiles_by_batch("m_t", HIDDEN, F32)
-        diffs = tiles_by_batch("diffs", HIDDEN, F32)
-        i_prime = tiles_by_batch("i_prime", HIDDEN, F32)
-        f_prime = tiles_by_batch("f_prime", HIDDEN, F32)
+        warm = keep.tile([P, 1], F32)
+        UNITS = N_HALVES * BATCH_TILES
+        sig_t = tiles("sig_t", N_HALVES, TILES_PER_BANK * BATCH, F32)
+        log_t = tiles("log_t", UNITS, N_TILE, F32)
+        m_less = tiles("m_less", BATCH_TILES, HIDDEN, F32)
+        f_less = tiles("f_less", UNITS, N_TILE, F32)
+        diff = tiles("diff", UNITS, N_TILE, F32)
+        m_t = tiles("m_t", UNITS, N_TILE, F32)
+        below = tiles("below", UNITS, N_TILE, F32)
+        above = tiles("above", UNITS, N_TILE, F32)
+        halves = [slice(nh * N_TILE, (nh + 1) * N_TILE) for nh in range(N_HALVES)]
 
+        nc.vector.memset(ln_guard[:], LN_GUARD)
+        nc.scalar.activation(out=warm[:], in_=ln_guard[:], func=ACT.Sigmoid)
         nc.vector.memset(ones[:], 1.0)
         nc.vector.memset(idle_rhs[:], 0.0)
-        nc.vector.memset(bias_rows[:].bitcast(I32), 0)
+        nc.vector.memset(bias_rows_f[:].bitcast(I32), 0)
+        nc.vector.memset(bias_rows_i[:].bitcast(I32), 0)
         for gate in (F_GATE, I_GATE):
             for planes in w_scales[gate]:
                 nc.vector.memset(planes[:].rearrange("p s n -> p (s n)").bitcast(I32), 0)
-        nc.vector.memset(ln_guard[:], LN_GUARD)
         make_identity(nc, ident[:])
 
         def load_rows(tiles_sb, source, bt):
             nc.sync.dma_start(out=tiles_sb[bt][:], in_=source[bt * P : (bt + 1) * P, :])
 
-        def load_weight(gate, operand, words, scales):
+        def load_scales(gate, operand, scales):
             for r in range(4):
                 nc.sync.dma_start(
                     out=w_scales[gate][operand][r : P : 32, :, :].bitcast(I32),
                     in_=scales[:, r : 16 : 4, :].rearrange("g q n -> q g n").bitcast(I32),
                 )
+
+        def load_words(gate, operand, words):
             nc.sync.dma_start(
                 out=w_words[gate][operand][:].bitcast(I32), in_=words.rearrange("g p c -> p g c").bitcast(I32)
             )
 
-        for bt in CHUNKS[0]:
-            load_rows(x_sb, x, bt)
-            load_rows(h_sb, h_prev, bt)
-        nc.sync.dma_start(out=bias_rows[0:1, :], in_=b_f.rearrange("(o n) -> o n", o=1))
+        def load_weight(gate, operand, words, scales):
+            load_scales(gate, operand, scales)
+            load_words(gate, operand, words)
+
+        def load_bias_rows():
+            nc.sync.dma_start(out=bias_rows_f[0:HIDDEN_TILES, :], in_=b_f.rearrange("(c p) -> c p", p=P))
+            nc.sync.dma_start(out=bias_rows_i[0:1, :], in_=b_i.rearrange("(o n) -> o n", o=1))
+
+        load_rows(x_sb, x, 0)
+        load_rows(x_sb, x, 1)
+        load_bias_rows()
+        load_rows(x_sb, x, 2)
+        load_rows(x_sb, x, 3)
+        load_rows(h_sb, h_prev, 0)
+        load_rows(h_sb, h_prev, 1)
+        load_rows(h_sb, h_prev, 2)
+        load_rows(h_sb, h_prev, 3)
         load_weight(F_GATE, 0, Wf_x_words, Wf_x_scales)
         load_weight(F_GATE, 1, Wf_h_words, Wf_h_scales)
-        for bt in CHUNKS[1]:
-            load_rows(x_sb, x, bt)
-            load_rows(h_sb, h_prev, bt)
+        load_rows(m_sb, m_prev, 0)
+        load_rows(m_sb, m_prev, 1)
+        load_rows(m_sb, m_prev, 2)
+        load_rows(m_sb, m_prev, 3)
         load_weight(I_GATE, 0, Wi_x_words, Wi_x_scales)
         load_weight(I_GATE, 1, Wi_h_words, Wi_h_scales)
-        for bt in range(BATCH_TILES):
-            load_rows(m_sb, m_prev, bt)
-        nc.sync.dma_start(out=bias_i_all[:], in_=b_i.partition_broadcast(P))
 
-        def keep_clock(count):
-            unread = psum_acc.tile([P, N_TILE], F32, tag="acc")
+        def keep_clock(target, count):
             for step in range(count):
-                nc.tensor.matmul(out=unread[:], lhsT=ones[:], rhs=idle_rhs[:], start=True, stop=True)
+                nc.tensor.matmul(out=target[:], lhsT=ones[:], rhs=idle_rhs[:], start=True, stop=True)
 
-        keep_clock(4)
+        groupeds = {}
+        f_accs = {}
+        i_accs = {}
+        logs = {}
 
-        def turn(act_sb, bt, copy_out):
+        def turn(act_sb, operand, bt, copy_out, dummies):
             row_words = act_sb[bt][:].bitcast(F32)
-            turned = psum_t.tile([P, GROUPS, 2, P], F32)
+            turned = acc_bank("turned")
+            keep_clock(turned, dummies)
             for g in range(GROUPS):
                 for u in range(2):
                     nc.tensor.transpose(
-                        out=turned[:, g, u, :],
+                        out=turned[:, (2 * g + u) * P : (2 * g + u + 1) * P],
                         in_=row_words[:, WORDS_PER_GROUP * g + u : WORDS_PER_GROUP * (g + 1) : 2],
                         identity=ident[:],
                     )
             grouped = stage.tile([P, GROUPS * P * 4], BF16, align_bytes=64)
             copy_out(
                 out=grouped[:].bitcast(F32).rearrange("p (g b u) -> p g b u", g=GROUPS, u=2),
-                in_=turned[:].rearrange("p g u b -> p g b u"),
+                in_=turned[:].rearrange("p (g u b) -> p g b u", g=GROUPS, u=2),
             )
-            return grouped
+            groupeds[operand, bt] = grouped
 
-        def quantise(grouped, bt, operand):
-            passes = slice(operand * GROUPS * P, (operand + 1) * GROUPS * P)
-            nc.vector.quantize_mx(out=a_codes[bt][:, passes].bitcast(FP8X4), scales=a_scales[bt][:, passes], in_=grouped[:])
-
-        def quantise_chunk(chunk, x_copy_out):
-            for bt in chunk:
-                grouped_x = turn(x_sb, bt, x_copy_out)
-                grouped_h = turn(h_sb, bt, nc.vector.tensor_copy)
-                keep_clock(2)
-                quantise(grouped_x, bt, 0)
-                quantise(grouped_h, bt, 1)
-
-        quantise_chunk(CHUNKS[0], nc.scalar.copy)
-
-        halves = [slice(nh * N_TILE, (nh + 1) * N_TILE) for nh in range(N_HALVES)]
-        whole = [slice(0, HIDDEN)]
-
-        for cols in halves:
-            spread = psum_acc.tile([P, N_TILE], F32, tag="acc")
-            nc.tensor.matmul(out=spread[:], lhsT=ones[:], rhs=bias_rows[:, cols], start=True, stop=True)
-            nc.scalar.copy(out=bias_f_all[:, cols], in_=spread[:])
-
-        def gate_products(gate, bt):
-            banks = [psum_acc.tile([P, N_TILE], F32, name="acc%d" % nh, tag="acc") for nh in range(N_HALVES)]
-            for ps in range(PASSES):
-                operand, g = divmod(ps, GROUPS)
-                for nh in range(N_HALVES):
-                    nc.tensor.matmul_mx(
-                        out=banks[nh][:],
-                        lhsT=a_codes[bt][:, ps * P : (ps + 1) * P].bitcast(FP8X4),
-                        lhsT_scale=a_scales[bt][:, ps * P : (ps + 1) * P],
-                        rhs=w_words[gate][operand][:, g, 2 * nh * N_TILE : 2 * (nh + 1) * N_TILE].bitcast(FP4X4),
-                        rhs_scale=w_scales[gate][operand][:, g, nh * N_TILE : (nh + 1) * N_TILE],
-                        start=(ps == 0),
-                        stop=(ps == PASSES - 1),
-                    )
-            return banks
-
-        def forget_sigmoids(chunk):
-            for bt in chunk:
-                banks = gate_products(F_GATE, bt)
-                f_aff = work.tile([P, HIDDEN], F32)
-                for nh, cols in enumerate(halves):
-                    nc.vector.tensor_tensor(out=f_aff[:, cols], in0=banks[nh][:], in1=bias_f_all[:, cols], op=ALU.add)
-                nc.scalar.activation(out=sig_f[bt][:], in_=f_aff[:], func=ACT.Sigmoid)
-
-        def logarithm(bt):
-            log_s = work.tile([P, HIDDEN], F32)
-            nc.scalar.activation(out=log_s[:], in_=sig_f[bt][:], func=ACT.Ln, bias=ln_guard[:, 0:1])
-            return log_s
-
-        def forget_path(bt, log_s):
-            for cols in whole:
-                nc.vector.scalar_tensor_tensor(
-                    out=f_path[bt][:, cols],
-                    in0=log_s[:, cols],
-                    scalar=LOG_FLOOR,
-                    in1=m_sb[bt][:, cols],
-                    op0=ALU.max,
-                    op1=ALU.add,
+        def quantise(operand, bt):
+            rows = slice(bt * P, (bt + 1) * P)
+            for g in range(GROUPS):
+                ps = operand * GROUPS + g
+                nc.vector.quantize_mx(
+                    out=a_codes[ps][:, rows].bitcast(FP8X4),
+                    scales=a_scales[ps][:, rows],
+                    in_=groupeds[operand, bt][:, g * K_PASS : (g + 1) * K_PASS],
                 )
 
-        def stabilise(bt, pieces, above_engine, m_t_first):
-            banks = gate_products(I_GATE, bt)
-            i_tilde = work.tile([P, HIDDEN], F32)
-            diff = diffs[bt]
-            for nh, cols in enumerate(halves):
-                nc.vector.tensor_tensor(out=i_tilde[:, cols], in0=banks[nh][:], in1=bias_i_all[:, cols], op=ALU.add)
-            if m_t_first:
-                for cols in halves:
-                    nc.vector.tensor_tensor(out=m_t[bt][:, cols], in0=i_tilde[:, cols], in1=f_path[bt][:, cols], op=ALU.max)
-                for cols in pieces:
-                    nc.sync.dma_start(out=out_0[bt * P : (bt + 1) * P, cols], in_=m_t[bt][:, cols])
+        def prepare_bias_f():
+            nc.vector.tensor_copy(out=ident_head[:], in_=ident[:, 0:HIDDEN_TILES])
+
+        def spread_bias_f():
+            spread = side_bank("spread_f")
+            nc.tensor.matmul(out=spread[:, 0:HIDDEN_TILES], lhsT=bias_rows_f[:], rhs=ident_head[:], start=True, stop=True)
+            nc.vector.tensor_copy(out=bias_f[:], in_=spread[:, 0:HIDDEN_TILES])
+
+        def spread_bias_i():
             for cols in halves:
-                nc.vector.tensor_tensor(out=diff[:, cols], in0=i_tilde[:, cols], in1=f_path[bt][:, cols], op=ALU.subtract)
-            for cols in halves:
-                nc.vector.tensor_scalar_min(out=below[bt][:, cols], in0=diff[:, cols], scalar1=0.0)
-            if above_engine == "vector":
-                for cols in halves:
-                    nc.vector.tensor_scalar_max(out=above[bt][:, cols], in0=diff[:, cols], scalar1=0.0)
-            elif above_engine == "scalar":
-                for cols in pieces:
-                    nc.scalar.activation(out=above[bt][:, cols], in_=diff[:, cols], func=ACT.Relu)
-            if not m_t_first:
-                for cols in halves:
-                    nc.vector.tensor_tensor(out=m_t[bt][:, cols], in0=i_tilde[:, cols], in1=f_path[bt][:, cols], op=ALU.max)
-                if bt != BATCH_TILES - 1:
-                    for cols in pieces:
-                        nc.sync.dma_start(out=out_0[bt * P : (bt + 1) * P, cols], in_=m_t[bt][:, cols])
+                spread = side_bank("spread_i")
+                nc.tensor.matmul(out=spread[:], lhsT=ones[:], rhs=bias_rows_i[:, cols], start=True, stop=True)
+                nc.scalar.copy(out=bias_i[:, cols], in_=spread[:])
 
-        def stabilise_pair(bt_a, bt_b, fillers):
-            tildes = {}
+        def forget_pass(ht, ps):
+            if ps == 0:
+                f_accs[ht] = acc_bank("f_acc%d" % ht)
+            operand, g = divmod(ps, GROUPS)
+            nc.tensor.matmul_mx(
+                out=f_accs[ht][:],
+                lhsT=w_words[F_GATE][operand][:, g, 2 * ht * P : 2 * (ht + 1) * P].bitcast(FP4X4),
+                lhsT_scale=w_scales[F_GATE][operand][:, g, ht * P : (ht + 1) * P],
+                rhs=a_codes[ps][:].bitcast(FP8X4),
+                rhs_scale=a_scales[ps][:],
+                start=(ps == 0),
+                stop=(ps == PASSES - 1),
+            )
 
-            def products_and_max(bt):
-                banks = gate_products(I_GATE, bt)
-                i_tilde = work.tile([P, HIDDEN], F32)
-                tildes[bt] = i_tilde
-                for nh, cols in enumerate(halves):
-                    nc.vector.tensor_tensor(out=i_tilde[:, cols], in0=banks[nh][:], in1=bias_i_all[:, cols], op=ALU.add)
-                for cols in halves:
-                    nc.vector.tensor_tensor(out=m_t[bt][:, cols], in0=i_tilde[:, cols], in1=f_path[bt][:, cols], op=ALU.max)
-                nc.sync.dma_start(out=out_0[bt * P : (bt + 1) * P, :], in_=m_t[bt][:])
-                nc.vector.tensor_tensor(out=diffs[bt][:], in0=i_tilde[:], in1=f_path[bt][:], op=ALU.subtract)
+        def forget_sigmoid(ht):
+            nh, t = divmod(ht, TILES_PER_BANK)
+            nc.scalar.activation(
+                out=sig_t[nh][:, t * BATCH : (t + 1) * BATCH], in_=f_accs[ht][:], func=ACT.Sigmoid, bias=bias_f[:, ht : ht + 1]
+            )
 
-            products_and_max(bt_a)
-            products_and_max(bt_b)
-            nc.vector.tensor_scalar_min(out=below[bt_a][:], in0=diffs[bt_a][:], scalar1=0.0)
-            nc.vector.tensor_scalar_min(out=below[bt_b][:], in0=diffs[bt_b][:], scalar1=0.0)
+        def input_products(unit):
+            nh, bt = divmod(unit, BATCH_TILES)
+            i_accs[unit] = acc_bank("i_acc%d" % unit)
+            for ps in range(PASSES):
+                operand, g = divmod(ps, GROUPS)
+                nc.tensor.matmul_mx(
+                    out=i_accs[unit][:],
+                    lhsT=a_codes[ps][:, bt * P : (bt + 1) * P].bitcast(FP8X4),
+                    lhsT_scale=a_scales[ps][:, bt * P : (bt + 1) * P],
+                    rhs=w_words[I_GATE][operand][:, g, 2 * nh * N_TILE : 2 * (nh + 1) * N_TILE].bitcast(FP4X4),
+                    rhs_scale=w_scales[I_GATE][operand][:, g, nh * N_TILE : (nh + 1) * N_TILE],
+                    start=(ps == 0),
+                    stop=(ps == PASSES - 1),
+                )
 
-        def exponentials(bt, pieces, relu_first=False):
-            rows = slice(bt * P, (bt + 1) * P)
-            if relu_first:
-                nc.scalar.activation(out=above[bt][:], in_=diffs[bt][:], func=ACT.Relu)
-            for cols in pieces:
-                nc.scalar.activation(out=i_prime[bt][:, cols], in_=below[bt][:, cols], func=ACT.Exp)
-                nc.sync.dma_start(out=out_1[rows, cols], in_=i_prime[bt][:, cols])
-            if bt == BATCH_TILES - 1:
-                for cols in pieces:
-                    nc.sync.dma_start(out=out_0[rows, cols], in_=m_t[bt][:, cols])
-            for cols in pieces:
-                nc.scalar.activation(out=f_prime[bt][:, cols], in_=above[bt][:, cols], func=ACT.Exp, scale=-1.0)
-                nc.sync.dma_start(out=out_2[rows, cols], in_=f_prime[bt][:, cols])
+        def logarithm(unit):
+            nh, bt = divmod(unit, BATCH_TILES)
+            nc.scalar.activation(
+                out=log_t[unit][:].rearrange("p (t b) -> p t b", b=P),
+                in_=sig_t[nh][:].rearrange("p (t b) -> p t b", b=BATCH)[:, :, bt * P : (bt + 1) * P],
+                func=ACT.Ln,
+                bias=ln_guard[:, 0:1],
+            )
 
-        forget_sigmoids(CHUNKS[0])
-        quantise_chunk(CHUNKS[1], nc.vector.tensor_copy)
-        first_logs = [logarithm(bt) for bt in CHUNKS[0]]
-        for bt_first, bt_second, log_s in zip(CHUNKS[0], CHUNKS[1], first_logs):
-            forget_sigmoids((bt_second,))
-            forget_path(bt_first, log_s)
-        stabilise_pair(CHUNKS[0][0], CHUNKS[0][1], ())
-        for bt in CHUNKS[1]:
-            forget_path(bt, logarithm(bt))
-        for bt in CHUNKS[0]:
-            exponentials(bt, whole, relu_first=True)
-        for bt in CHUNKS[1]:
-            pieces = halves if bt == BATCH_TILES - 1 else whole
-            stabilise(bt, pieces, "vector" if bt == BATCH_TILES - 1 else "scalar", False)
-            exponentials(bt, pieces)
+        def turn_back(unit):
+            logs[unit] = side_bank("log%d" % unit)
+            for t in range(TILES_PER_BANK):
+                nc.tensor.transpose(
+                    out=logs[unit][:, t * P : (t + 1) * P], in_=log_t[unit][:, t * P : (t + 1) * P], identity=ident[:]
+                )
+
+        def less_bias(engine, bt):
+            engine.tensor_tensor(out=m_less[bt][:], in0=m_sb[bt][:], in1=bias_i[:], op=ALU.subtract)
+
+        def forget_path(unit):
+            nh, bt = divmod(unit, BATCH_TILES)
+            nc.vector.scalar_tensor_tensor(
+                out=f_less[unit][:], in0=logs[unit][:], scalar=LOG_FLOOR, in1=m_less[bt][:, halves[nh]], op0=ALU.max, op1=ALU.add
+            )
+
+        def against_path(out_tiles, unit, op):
+            nc.vector.tensor_tensor(out=out_tiles[unit][:], in0=i_accs[unit][:], in1=f_less[unit][:], op=op)
+
+        def add_bias(engine, unit):
+            nh, bt = divmod(unit, BATCH_TILES)
+            engine.tensor_tensor(out=m_t[unit][:], in0=m_t[unit][:], in1=bias_i[:, halves[nh]], op=ALU.add)
+
+        def clip_below(unit):
+            nc.vector.tensor_scalar_min(out=below[unit][:], in0=diff[unit][:], scalar1=0.0)
+
+        def clip_above(unit):
+            nc.vector.tensor_scalar_max(out=above[unit][:], in0=diff[unit][:], scalar1=0.0)
+
+        def relu_above(unit):
+            nc.scalar.activation(out=above[unit][:], in_=diff[unit][:], func=ACT.Relu)
+
+        def store(out, source, unit):
+            nh, bt = divmod(unit, BATCH_TILES)
+            nc.sync.dma_start(out=out[bt * P : (bt + 1) * P, halves[nh]], in_=source[unit][:])
+
+        def exp_below(unit):
+            nc.scalar.activation(out=below[unit][:], in_=below[unit][:], func=ACT.Exp)
+            store(out_1, below, unit)
+
+        def exp_above(unit):
+            nc.scalar.activation(out=above[unit][:], in_=above[unit][:], func=ACT.Exp, scale=-1.0)
+            store(out_2, above, unit)
+
+        keep_clock(acc_bank("idle"), 4)
+        prepare_bias_f()
+        turn(x_sb, 0, 0, nc.scalar.copy, 0)
+        quantise(0, 0)
+        turn(x_sb, 0, 1, nc.scalar.copy, 0)
+        quantise(0, 1)
+        spread_bias_f()
+        turn(x_sb, 0, 2, nc.scalar.copy, 0)
+        quantise(0, 2)
+        turn(x_sb, 0, 3, nc.scalar.copy, 0)
+        quantise(0, 3)
+        turn(h_sb, 1, 0, nc.scalar.copy, 2)
+        quantise(1, 0)
+        turn(h_sb, 1, 1, nc.scalar.copy, 0)
+        quantise(1, 1)
+        turn(h_sb, 1, 2, nc.scalar.copy, 0)
+        quantise(1, 2)
+        turn(h_sb, 1, 3, nc.scalar.copy, 0)
+        quantise(1, 3)
+        spread_bias_i()
+        forget_pass(0, 0)
+        forget_pass(1, 0)
+        forget_pass(2, 0)
+        forget_pass(3, 0)
+        forget_pass(0, 1)
+        forget_pass(1, 1)
+        forget_pass(2, 1)
+        forget_pass(3, 1)
+        forget_pass(0, 2)
+        forget_pass(0, 3)
+        forget_sigmoid(0)
+        forget_pass(1, 2)
+        forget_pass(1, 3)
+        forget_sigmoid(1)
+        forget_pass(2, 2)
+        forget_pass(2, 3)
+        forget_sigmoid(2)
+        forget_pass(3, 2)
+        forget_pass(3, 3)
+        forget_sigmoid(3)
+        less_bias(nc.vector, 0)
+        less_bias(nc.vector, 1)
+        less_bias(nc.vector, 2)
+        less_bias(nc.vector, 3)
+        logarithm(0)
+        logarithm(1)
+        logarithm(2)
+        logarithm(3)
+        forget_pass(4, 0)
+        forget_pass(4, 1)
+        forget_pass(4, 2)
+        forget_pass(4, 3)
+        forget_pass(5, 0)
+        forget_pass(5, 1)
+        forget_pass(5, 2)
+        forget_pass(5, 3)
+        input_products(0)
+        turn_back(0)
+        forget_path(0)
+        input_products(1)
+        against_path(diff, 0, ALU.subtract)
+        against_path(m_t, 0, ALU.max)
+        clip_below(0)
+        clip_above(0)
+        add_bias(nc.gpsimd, 0)
+        turn_back(1)
+        forget_path(1)
+        forget_pass(6, 0)
+        forget_pass(6, 1)
+        forget_pass(6, 2)
+        forget_pass(6, 3)
+        forget_pass(7, 0)
+        forget_pass(7, 1)
+        forget_pass(7, 2)
+        forget_pass(7, 3)
+        against_path(diff, 1, ALU.subtract)
+        against_path(m_t, 1, ALU.max)
+        clip_below(1)
+        clip_above(1)
+        add_bias(nc.gpsimd, 1)
+        forget_sigmoid(4)
+        forget_sigmoid(5)
+        forget_sigmoid(6)
+        forget_sigmoid(7)
+        store(out_0, m_t, 0)
+        store(out_0, m_t, 1)
+        turn_back(2)
+        forget_path(2)
+        turn_back(3)
+        forget_path(3)
+        input_products(2)
+        input_products(3)
+        input_products(4)
+        input_products(5)
+        logarithm(4)
+        logarithm(5)
+        logarithm(6)
+        logarithm(7)
+        against_path(diff, 2, ALU.subtract)
+        against_path(m_t, 2, ALU.max)
+        clip_below(2)
+        clip_above(2)
+        add_bias(nc.gpsimd, 2)
+        store(out_0, m_t, 2)
+        against_path(diff, 3, ALU.subtract)
+        against_path(m_t, 3, ALU.max)
+        clip_below(3)
+        clip_above(3)
+        add_bias(nc.gpsimd, 3)
+        store(out_0, m_t, 3)
+        turn_back(4)
+        forget_path(4)
+        turn_back(5)
+        forget_path(5)
+        input_products(6)
+        input_products(7)
+        exp_below(0)
+        exp_above(0)
+        exp_below(1)
+        exp_above(1)
+        exp_below(2)
+        exp_above(2)
+        against_path(diff, 4, ALU.subtract)
+        against_path(m_t, 4, ALU.max)
+        clip_below(4)
+        clip_above(4)
+        add_bias(nc.gpsimd, 4)
+        store(out_0, m_t, 4)
+        exp_below(3)
+        exp_above(3)
+        turn_back(6)
+        forget_path(6)
+        against_path(diff, 5, ALU.subtract)
+        against_path(m_t, 5, ALU.max)
+        clip_below(5)
+        clip_above(5)
+        add_bias(nc.gpsimd, 5)
+        turn_back(7)
+        forget_path(7)
+        exp_below(4)
+        exp_above(4)
+        store(out_0, m_t, 5)
+        against_path(diff, 6, ALU.subtract)
+        against_path(m_t, 6, ALU.max)
+        clip_below(6)
+        clip_above(6)
+        add_bias(nc.gpsimd, 6)
+        exp_below(5)
+        exp_above(5)
+        store(out_0, m_t, 6)
+        exp_below(6)
+        exp_above(6)
+        against_path(diff, 7, ALU.subtract)
+        against_path(m_t, 7, ALU.max)
+        clip_below(7)
+        clip_above(7)
+        add_bias(nc.vector, 7)
+        exp_below(7)
+        store(out_0, m_t, 7)
+        exp_above(7)

import math
from contextlib import ExitStack

import concourse.mybir as mybir
from concourse.masks import make_identity

F32 = mybir.dt.float32
BF16 = mybir.dt.bfloat16
I32 = mybir.dt.int32
U32 = mybir.dt.uint32
U8 = mybir.dt.uint8
FP8X4 = mybir.dt.float8_e4m3fn_x4
FP4X4 = mybir.dt.float4_e2m1fn_x4
ACT = mybir.ActivationFunctionType
ALU = mybir.AluOpType

P = 128
BATCH = 512
FEATURES = 1024
HIDDEN = 1024
K_PASS = 4 * P
BATCH_TILES = BATCH // P
HIDDEN_TILES = HIDDEN // P
GROUPS = FEATURES // K_PASS
PASSES = 2 * GROUPS
N_TILE = 512
N_HALVES = HIDDEN // N_TILE
TILES_PER_BANK = N_TILE // P
WORDS_PER_GROUP = K_PASS // 2
F_GATE, I_GATE = 0, 1

SIGMOID_FLOOR = 1e-8
LOG_FLOOR = math.log(SIGMOID_FLOOR)
LN_GUARD = 1e-18

FLOPS = 2 * BATCH * (2 * FEATURES) * (2 * HIDDEN)


def tile_slstmlayer_pa_kernel(
    tc,
    x,
    h_prev,
    m_prev,
    Wi_x_words,
    Wi_x_scales,
    b_i,
    Wi_h_words,
    Wi_h_scales,
    Wf_x_words,
    Wf_x_scales,
    b_f,
    Wf_h_words,
    Wf_h_scales,
    out_0,
    out_1,
    out_2,
):
    nc = tc.nc
    with ExitStack() as ctx:
        keep = ctx.enter_context(tc.tile_pool(name="keep", bufs=1))
        stage = ctx.enter_context(tc.tile_pool(name="stage", bufs=4))
        psum_acc = ctx.enter_context(tc.psum_pool(name="psum_acc", bufs=6))
        psum_side = ctx.enter_context(tc.psum_pool(name="psum_side", bufs=2))
        ctx.enter_context(tc.manual_schedule())

        def acc_bank(name):
            return psum_acc.tile([P, N_TILE], F32, name=name, tag="acc")

        def side_bank(name):
            return psum_side.tile([P, N_TILE], F32, name=name, tag="side")

        def tiles(name, count, width, dtype):
            return [keep.tile([P, width], dtype, name="%s%d" % (name, j), align_bytes=64) for j in range(count)]

        x_sb = tiles("x_sb", BATCH_TILES, FEATURES, BF16)
        h_sb = tiles("h_sb", BATCH_TILES, FEATURES, BF16)
        m_sb = tiles("m_sb", BATCH_TILES, HIDDEN, BF16)
        w_words = [
            [keep.tile([P, GROUPS, 2 * HIDDEN], U8, name="w_words%d%d" % (gate, o), align_bytes=64) for o in range(2)]
            for gate in range(2)
        ]
        w_scales = [
            [keep.tile([P, GROUPS, HIDDEN], U8, name="w_scales%d%d" % (gate, o), align_bytes=64) for o in range(2)]
            for gate in range(2)
        ]
        a_codes = tiles("a_codes", PASSES, BATCH, U32)
        a_scales = tiles("a_scales", PASSES, BATCH, U8)
        bias_rows_f = keep.tile([P, P], BF16)
        bias_rows_i = keep.tile([P, HIDDEN], BF16)
        bias_f = keep.tile([P, HIDDEN_TILES], F32)
        bias_i = keep.tile([P, HIDDEN], F32)
        ones = keep.tile([P, P], BF16)
        idle_rhs = keep.tile([P, N_TILE], BF16)
        ident = keep.tile([P, P], F32)
        ident_head = keep.tile([P, HIDDEN_TILES], BF16)
        ln_guard = keep.tile([P, 1], F32)
        warm = keep.tile([P, 1], F32)
        UNITS = N_HALVES * BATCH_TILES
        sig_t = tiles("sig_t", N_HALVES, TILES_PER_BANK * BATCH, F32)
        log_t = tiles("log_t", UNITS, N_TILE, F32)
        m_less = tiles("m_less", BATCH_TILES, HIDDEN, F32)
        f_less = tiles("f_less", UNITS, N_TILE, F32)
        diff = tiles("diff", UNITS, N_TILE, F32)
        m_t = tiles("m_t", UNITS, N_TILE, F32)
        below = tiles("below", UNITS, N_TILE, F32)
        above = tiles("above", UNITS, N_TILE, F32)
        halves = [slice(nh * N_TILE, (nh + 1) * N_TILE) for nh in range(N_HALVES)]

        nc.vector.memset(ln_guard[:], LN_GUARD)
        nc.scalar.activation(out=warm[:], in_=ln_guard[:], func=ACT.Sigmoid)
        nc.vector.memset(ones[:], 1.0)
        nc.vector.memset(idle_rhs[:], 0.0)
        nc.vector.memset(bias_rows_f[:].bitcast(I32), 0)
        nc.vector.memset(bias_rows_i[:].bitcast(I32), 0)
        for gate in (F_GATE, I_GATE):
            for planes in w_scales[gate]:
                nc.vector.memset(planes[:].rearrange("p s n -> p (s n)").bitcast(I32), 0)
        make_identity(nc, ident[:])

        def load_rows(tiles_sb, source, bt):
            nc.sync.dma_start(out=tiles_sb[bt][:], in_=source[bt * P : (bt + 1) * P, :])

        def load_scales(gate, operand, scales):
            for r in range(4):
                nc.sync.dma_start(
                    out=w_scales[gate][operand][r : P : 32, :, :].bitcast(I32),
                    in_=scales[:, r : 16 : 4, :].rearrange("g q n -> q g n").bitcast(I32),
                )

        def load_words(gate, operand, words):
            nc.sync.dma_start(
                out=w_words[gate][operand][:].bitcast(I32), in_=words.rearrange("g p c -> p g c").bitcast(I32)
            )

        def load_weight(gate, operand, words, scales):
            load_scales(gate, operand, scales)
            load_words(gate, operand, words)

        def load_bias_rows():
            nc.sync.dma_start(out=bias_rows_f[0:HIDDEN_TILES, :], in_=b_f.rearrange("(c p) -> c p", p=P))
            nc.sync.dma_start(out=bias_rows_i[0:1, :], in_=b_i.rearrange("(o n) -> o n", o=1))

        load_rows(x_sb, x, 0)
        load_rows(x_sb, x, 1)
        load_bias_rows()
        load_rows(x_sb, x, 2)
        load_rows(x_sb, x, 3)
        load_rows(h_sb, h_prev, 0)
        load_rows(h_sb, h_prev, 1)
        load_rows(h_sb, h_prev, 2)
        load_rows(h_sb, h_prev, 3)
        load_weight(F_GATE, 0, Wf_x_words, Wf_x_scales)
        load_weight(F_GATE, 1, Wf_h_words, Wf_h_scales)
        load_rows(m_sb, m_prev, 0)
        load_rows(m_sb, m_prev, 1)
        load_rows(m_sb, m_prev, 2)
        load_rows(m_sb, m_prev, 3)
        load_weight(I_GATE, 0, Wi_x_words, Wi_x_scales)
        load_weight(I_GATE, 1, Wi_h_words, Wi_h_scales)

        def keep_clock(target, count):
            for step in range(count):
                nc.tensor.matmul(out=target[:], lhsT=ones[:], rhs=idle_rhs[:], start=True, stop=True)

        groupeds = {}
        f_accs = {}
        i_accs = {}
        logs = {}

        def turn(act_sb, operand, bt, copy_out, dummies):
            row_words = act_sb[bt][:].bitcast(F32)
            turned = acc_bank("turned")
            keep_clock(turned, dummies)
            for g in range(GROUPS):
                for u in range(2):
                    nc.tensor.transpose(
                        out=turned[:, (2 * g + u) * P : (2 * g + u + 1) * P],
                        in_=row_words[:, WORDS_PER_GROUP * g + u : WORDS_PER_GROUP * (g + 1) : 2],
                        identity=ident[:],
                    )
            grouped = stage.tile([P, GROUPS * P * 4], BF16, align_bytes=64)
            copy_out(
                out=grouped[:].bitcast(F32).rearrange("p (g b u) -> p g b u", g=GROUPS, u=2),
                in_=turned[:].rearrange("p (g u b) -> p g b u", g=GROUPS, u=2),
            )
            groupeds[operand, bt] = grouped

        def quantise(operand, bt):
            rows = slice(bt * P, (bt + 1) * P)
            for g in range(GROUPS):
                ps = operand * GROUPS + g
                nc.vector.quantize_mx(
                    out=a_codes[ps][:, rows].bitcast(FP8X4),
                    scales=a_scales[ps][:, rows],
                    in_=groupeds[operand, bt][:, g * K_PASS : (g + 1) * K_PASS],
                )

        def prepare_bias_f():
            nc.vector.tensor_copy(out=ident_head[:], in_=ident[:, 0:HIDDEN_TILES])

        def spread_bias_f():
            spread = side_bank("spread_f")
            nc.tensor.matmul(out=spread[:, 0:HIDDEN_TILES], lhsT=bias_rows_f[:], rhs=ident_head[:], start=True, stop=True)
            nc.vector.tensor_copy(out=bias_f[:], in_=spread[:, 0:HIDDEN_TILES])

        def spread_bias_i():
            for cols in halves:
                spread = side_bank("spread_i")
                nc.tensor.matmul(out=spread[:], lhsT=ones[:], rhs=bias_rows_i[:, cols], start=True, stop=True)
                nc.scalar.copy(out=bias_i[:, cols], in_=spread[:])

        def forget_pass(ht, ps):
            if ps == 0:
                f_accs[ht] = acc_bank("f_acc%d" % ht)
            operand, g = divmod(ps, GROUPS)
            nc.tensor.matmul_mx(
                out=f_accs[ht][:],
                lhsT=w_words[F_GATE][operand][:, g, 2 * ht * P : 2 * (ht + 1) * P].bitcast(FP4X4),
                lhsT_scale=w_scales[F_GATE][operand][:, g, ht * P : (ht + 1) * P],
                rhs=a_codes[ps][:].bitcast(FP8X4),
                rhs_scale=a_scales[ps][:],
                start=(ps == 0),
                stop=(ps == PASSES - 1),
            )

        def forget_sigmoid(ht):
            nh, t = divmod(ht, TILES_PER_BANK)
            nc.scalar.activation(
                out=sig_t[nh][:, t * BATCH : (t + 1) * BATCH], in_=f_accs[ht][:], func=ACT.Sigmoid, bias=bias_f[:, ht : ht + 1]
            )

        def input_products(unit):
            nh, bt = divmod(unit, BATCH_TILES)
            i_accs[unit] = acc_bank("i_acc%d" % unit)
            for ps in range(PASSES):
                operand, g = divmod(ps, GROUPS)
                nc.tensor.matmul_mx(
                    out=i_accs[unit][:],
                    lhsT=a_codes[ps][:, bt * P : (bt + 1) * P].bitcast(FP8X4),
                    lhsT_scale=a_scales[ps][:, bt * P : (bt + 1) * P],
                    rhs=w_words[I_GATE][operand][:, g, 2 * nh * N_TILE : 2 * (nh + 1) * N_TILE].bitcast(FP4X4),
                    rhs_scale=w_scales[I_GATE][operand][:, g, nh * N_TILE : (nh + 1) * N_TILE],
                    start=(ps == 0),
                    stop=(ps == PASSES - 1),
                )

        def logarithm(unit):
            nh, bt = divmod(unit, BATCH_TILES)
            nc.scalar.activation(
                out=log_t[unit][:].rearrange("p (t b) -> p t b", b=P),
                in_=sig_t[nh][:].rearrange("p (t b) -> p t b", b=BATCH)[:, :, bt * P : (bt + 1) * P],
                func=ACT.Ln,
                bias=ln_guard[:, 0:1],
            )

        def turn_back(unit):
            logs[unit] = side_bank("log%d" % unit)
            for t in range(TILES_PER_BANK):
                nc.tensor.transpose(
                    out=logs[unit][:, t * P : (t + 1) * P], in_=log_t[unit][:, t * P : (t + 1) * P], identity=ident[:]
                )

        def less_bias(engine, bt):
            engine.tensor_tensor(out=m_less[bt][:], in0=m_sb[bt][:], in1=bias_i[:], op=ALU.subtract)

        def forget_path(unit):
            nh, bt = divmod(unit, BATCH_TILES)
            nc.vector.scalar_tensor_tensor(
                out=f_less[unit][:], in0=logs[unit][:], scalar=LOG_FLOOR, in1=m_less[bt][:, halves[nh]], op0=ALU.max, op1=ALU.add
            )

        def against_path(out_tiles, unit, op):
            nc.vector.tensor_tensor(out=out_tiles[unit][:], in0=i_accs[unit][:], in1=f_less[unit][:], op=op)

        def add_bias(engine, unit):
            nh, bt = divmod(unit, BATCH_TILES)
            engine.tensor_tensor(out=m_t[unit][:], in0=m_t[unit][:], in1=bias_i[:, halves[nh]], op=ALU.add)

        def clip_below(unit):
            nc.vector.tensor_scalar_min(out=below[unit][:], in0=diff[unit][:], scalar1=0.0)

        def clip_above(unit):
            nc.vector.tensor_scalar_max(out=above[unit][:], in0=diff[unit][:], scalar1=0.0)

        def relu_above(unit):
            nc.scalar.activation(out=above[unit][:], in_=diff[unit][:], func=ACT.Relu)

        def store(out, source, unit):
            nh, bt = divmod(unit, BATCH_TILES)
            nc.sync.dma_start(out=out[bt * P : (bt + 1) * P, halves[nh]], in_=source[unit][:])

        def exp_below(unit):
            nc.scalar.activation(out=below[unit][:], in_=below[unit][:], func=ACT.Exp)
            store(out_1, below, unit)

        def exp_above(unit):
            nc.scalar.activation(out=above[unit][:], in_=above[unit][:], func=ACT.Exp, scale=-1.0)
            store(out_2, above, unit)

        keep_clock(acc_bank("idle"), 4)
        prepare_bias_f()
        turn(x_sb, 0, 0, nc.scalar.copy, 0)
        quantise(0, 0)
        turn(x_sb, 0, 1, nc.scalar.copy, 0)
        quantise(0, 1)
        spread_bias_f()
        turn(x_sb, 0, 2, nc.scalar.copy, 0)
        quantise(0, 2)
        turn(x_sb, 0, 3, nc.scalar.copy, 0)
        quantise(0, 3)
        turn(h_sb, 1, 0, nc.scalar.copy, 2)
        quantise(1, 0)
        turn(h_sb, 1, 1, nc.scalar.copy, 0)
        quantise(1, 1)
        turn(h_sb, 1, 2, nc.scalar.copy, 0)
        quantise(1, 2)
        turn(h_sb, 1, 3, nc.scalar.copy, 0)
        quantise(1, 3)
        spread_bias_i()
        forget_pass(0, 0)
        forget_pass(1, 0)
        forget_pass(2, 0)
        forget_pass(3, 0)
        forget_pass(0, 1)
        forget_pass(1, 1)
        forget_pass(2, 1)
        forget_pass(3, 1)
        forget_pass(0, 2)
        forget_pass(0, 3)
        forget_sigmoid(0)
        forget_pass(1, 2)
        forget_pass(1, 3)
        forget_sigmoid(1)
        forget_pass(2, 2)
        forget_pass(2, 3)
        forget_sigmoid(2)
        forget_pass(3, 2)
        forget_pass(3, 3)
        forget_sigmoid(3)
        less_bias(nc.vector, 0)
        less_bias(nc.vector, 1)
        less_bias(nc.vector, 2)
        less_bias(nc.vector, 3)
        logarithm(0)
        logarithm(1)
        logarithm(2)
        logarithm(3)
        forget_pass(4, 0)
        forget_pass(4, 1)
        forget_pass(4, 2)
        forget_pass(4, 3)
        forget_pass(5, 0)
        forget_pass(5, 1)
        forget_pass(5, 2)
        forget_pass(5, 3)
        input_products(0)
        turn_back(0)
        forget_path(0)
        input_products(1)
        against_path(diff, 0, ALU.subtract)
        against_path(m_t, 0, ALU.max)
        clip_below(0)
        clip_above(0)
        add_bias(nc.gpsimd, 0)
        turn_back(1)
        forget_path(1)
        forget_pass(6, 0)
        forget_pass(6, 1)
        forget_pass(6, 2)
        forget_pass(6, 3)
        forget_pass(7, 0)
        forget_pass(7, 1)
        forget_pass(7, 2)
        forget_pass(7, 3)
        against_path(diff, 1, ALU.subtract)
        against_path(m_t, 1, ALU.max)
        clip_below(1)
        clip_above(1)
        add_bias(nc.gpsimd, 1)
        forget_sigmoid(4)
        forget_sigmoid(5)
        forget_sigmoid(6)
        forget_sigmoid(7)
        store(out_0, m_t, 0)
        store(out_0, m_t, 1)
        turn_back(2)
        forget_path(2)
        turn_back(3)
        forget_path(3)
        input_products(2)
        input_products(3)
        input_products(4)
        input_products(5)
        logarithm(4)
        logarithm(5)
        logarithm(6)
        logarithm(7)
        against_path(diff, 2, ALU.subtract)
        against_path(m_t, 2, ALU.max)
        clip_below(2)
        clip_above(2)
        add_bias(nc.gpsimd, 2)
        store(out_0, m_t, 2)
        against_path(diff, 3, ALU.subtract)
        against_path(m_t, 3, ALU.max)
        clip_below(3)
        clip_above(3)
        add_bias(nc.gpsimd, 3)
        store(out_0, m_t, 3)
        turn_back(4)
        forget_path(4)
        turn_back(5)
        forget_path(5)
        input_products(6)
        input_products(7)
        exp_below(0)
        exp_above(0)
        exp_below(1)
        exp_above(1)
        exp_below(2)
        exp_above(2)
        against_path(diff, 4, ALU.subtract)
        against_path(m_t, 4, ALU.max)
        clip_below(4)
        clip_above(4)
        add_bias(nc.gpsimd, 4)
        store(out_0, m_t, 4)
        exp_below(3)
        exp_above(3)
        turn_back(6)
        forget_path(6)
        against_path(diff, 5, ALU.subtract)
        against_path(m_t, 5, ALU.max)
        clip_below(5)
        clip_above(5)
        add_bias(nc.gpsimd, 5)
        turn_back(7)
        forget_path(7)
        exp_below(4)
        exp_above(4)
        store(out_0, m_t, 5)
        against_path(diff, 6, ALU.subtract)
        against_path(m_t, 6, ALU.max)
        clip_below(6)
        clip_above(6)
        add_bias(nc.gpsimd, 6)
        exp_below(5)
        exp_above(5)
        store(out_0, m_t, 6)
        exp_below(6)
        exp_above(6)
        against_path(diff, 7, ALU.subtract)
        against_path(m_t, 7, ALU.max)
        clip_below(7)
        clip_above(7)
        add_bias(nc.vector, 7)
        exp_below(7)
        store(out_0, m_t, 7)
        exp_above(7)
